import numpy as np
import ml_dtypes


def mxq(x, axis, fmt="e4m3"):
    dtype, down = {"e4m3": (ml_dtypes.float8_e4m3fn, 7), "e5m2": (ml_dtypes.float8_e5m2, 14)}[fmt]
    v = np.moveaxis(np.asarray(x, np.float32).astype(ml_dtypes.bfloat16).astype(np.float64), axis, -1)
    blocks = v.reshape(v.shape[:-1] + (-1, 32))
    amax = np.abs(blocks).max(-1, keepdims=True)
    byte = np.maximum(np.where(amax > 0, np.frexp(amax)[1] - 1 + 127, 0) - down, 1)
    scale = np.exp2(byte - 127.0)
    codes = (blocks / scale).astype(np.float32).astype(dtype).astype(np.float64)
    return np.moveaxis((codes * scale).reshape(v.shape), -1, axis)


WIDE = False


def mx_kscale(k):
    if not WIDE:
        return np.ones(k)
    levels = np.array([10, -10, 5, -5, 0])
    if k % 512:
        return np.exp2(np.random.permutation(np.resize(levels, k // 32))).repeat(32)
    a = np.empty((k // 512, 16))
    for p in range(k // 512):
        a[p, :8] = np.random.permutation(np.resize(levels, 8))
        for g in range(8):
            far = levels[np.abs(levels - a[p, g]) >= 10]
            a[p, g + 8] = far[np.random.randint(len(far))]
    return np.exp2(a.ravel()).repeat(32)


BF16 = ml_dtypes.bfloat16


def bf(x):
    return np.asarray(x, np.float32).astype(BF16)


def f64(x):
    return np.asarray(x).astype(np.float64)


B, Q, D = 256, 2048, 512
COMBOS = ((0, 1), (0, 2), (0, 3), (1, 0), (1, 2), (2, 0), (2, 1), (3, 0))
T = 0.07
V = 1 + max(max(c) for c in COMBOS)


def setup_inputs():
    s = mx_kscale(D)
    c = np.mean(s * s)
    shared = np.random.standard_normal((B, D))
    d = {}
    for v in range(V):
        gain = np.random.uniform(0.6, 1.6, (B, 1))
        own = np.random.standard_normal((B, D))
        d["x%d" % v] = bf((np.sqrt(0.1) * shared + np.sqrt(0.9) * own) * gain * s)
    for v in range(V):
        d["mem%d" % v] = bf(np.random.standard_normal((Q, D)) * c / s)
    return d


def core(x0, x1, x2, x3, mem0, mem1, mem2, mem3):
    X = [f64(x0), f64(x1), f64(x2), f64(x3)]
    Mem = [f64(mem0), f64(mem1), f64(mem2), f64(mem3)]
    Xn = [np.sqrt(np.sum(x * x, axis=1, keepdims=True)) for x in X]
    Xq = [mxq(x, 1, "e4m3") for x in X]
    Mq = [mxq(m, 1, "e4m3") for m in Mem]
    outs = []
    for i, j in COMBOS:
        self_dot = np.sum(X[i] * X[j], axis=1, keepdims=True)
        mem_dot = Xq[i] @ Mq[j].T
        logits = np.concatenate([self_dot, mem_dot], axis=1)
        outs.append(np.exp(logits / (Xn[i] * Xn[j]) / T))
    return np.stack(outs)


def e4m3fn_bytes(y):
    return np.clip(np.asarray(y, np.float64), -448.0, 448.0).astype(np.float32).astype(ml_dtypes.float8_e4m3fn).view(np.uint8)


def reference(x0, x1, x2, x3, mem0, mem1, mem2, mem3):
    out = core(x0, x1, x2, x3, mem0, mem1, mem2, mem3)
    s = np.max(np.abs(out), axis=-1, keepdims=True) / 448.0
    return out, e4m3fn_bytes(out / s)

@@ -1,0 +1,306 @@
+from contextlib import ExitStack
+
+import concourse.mybir as mybir
+from concourse.masks import make_identity
+
+F32 = mybir.dt.float32
+BF16 = mybir.dt.bfloat16
+U32 = mybir.dt.uint32
+U8 = mybir.dt.uint8
+FP8X4 = mybir.dt.float8_e4m3fn_x4
+FP8 = mybir.dt.float8_e4m3fn
+ALU = mybir.AluOpType
+ACT = mybir.ActivationFunctionType
+AX = mybir.AxisListType
+
+B, Q, D = 256, 2048, 512
+COMBOS = ((0, 1), (0, 2), (0, 3), (1, 0), (1, 2), (2, 0), (2, 1), (3, 0))
+TEMP = 0.07
+FLOPS = 2 * len(COMBOS) * B * Q * D
+
+P = 128
+NT = 512
+W = 1 + Q
+PAIRS = ((0, 1), (0, 2), (0, 3), (1, 2))
+BANK_ORDER = (0, 1, 2, 3)
+
+
+def v_share(u, n_units, n_preps):
+    if u == n_units - 1:
+        return 1344
+    if u == n_units - 2:
+        return 0
+    if u + 2 < n_preps:
+        return 1728
+    return 1408
+
+
+def tile_memorymoco_pa_kernel(tc, x0, x1, x2, x3, mem0, mem1, mem2, mem3, out_0, out_1):
+    nc = tc.nc
+    xs = (x0, x1, x2, x3)
+    mems = (mem0, mem1, mem2, mem3)
+
+    with ExitStack() as ctx:
+        const = ctx.enter_context(tc.tile_pool(name="const", bufs=1))
+        raw = ctx.enter_context(tc.tile_pool(name="raw", bufs=1))
+        keep = ctx.enter_context(tc.tile_pool(name="keep", bufs=1))
+        grp = ctx.enter_context(tc.tile_pool(name="grp", bufs=3))
+        tpool = ctx.enter_context(tc.tile_pool(name="tpool", bufs=6))
+        opool = ctx.enter_context(tc.tile_pool(name="opool", bufs=4))
+        small = ctx.enter_context(tc.tile_pool(name="small", bufs=4))
+        tps = ctx.enter_context(tc.psum_pool(name="tps", bufs=2))
+        psum = ctx.enter_context(tc.psum_pool(name="psum", bufs=6))
+
+        ident = const.tile([P, P], F32, name="ident")
+        make_identity(nc, ident[:])
+        mhalf = const.tile([P, 4], F32, name="mhalf")
+        nc.gpsimd.memset(mhalf[:], -0.5)
+        zero = const.tile([P, 1], F32, name="zero")
+        nc.vector.memset(zero[:], 0.0)
+        warm = const.tile([P, 1], F32, name="warm")
+        nc.scalar.activation(out=warm[:], in_=zero[:], func=ACT.Exp)
+
+        xraw = {}
+        mraw = {}
+
+        def load_view(v):
+            xraw[v] = raw.tile([P, 2, D], BF16, name="xraw%d" % v)
+            nc.sync.dma_start(out=xraw[v][:], in_=xs[v].rearrange("(m p) k -> p m k", p=P))
+
+        def load_chunk(j, c):
+            mraw[(j, c)] = raw.tile([P, 4, D], BF16, name="mraw%d_%d" % (j, c))
+            nc.sync.dma_start(
+                out=mraw[(j, c)][:], in_=mems[j][NT * c : NT * (c + 1), :].rearrange("(a p) k -> p a k", p=P)
+            )
+
+        load_view(1)
+        load_view(0)
+        load_chunk(BANK_ORDER[0], 0)
+        load_chunk(BANK_ORDER[0], 1)
+        load_view(2)
+        load_view(3)
+        load_chunk(BANK_ORDER[0], 2)
+        load_chunk(BANK_ORDER[0], 3)
+        for j in BANK_ORDER[1:]:
+            for c in range(4):
+                load_chunk(j, c)
+
+        gx = {}
+        xc = {}
+        xsc = {}
+        mc = {}
+        msc = {}
+        for v in range(4):
+            gx[v] = keep.tile([P, 4 * B], BF16, name="gx%d" % v, align_bytes=64)
+            xc[v] = keep.tile([P, B], U32, name="xc%d" % v, align_bytes=64)
+            xsc[v] = keep.tile([P, B], U8, name="xsc%d" % v, align_bytes=64)
+            mc[v] = keep.tile([P, Q], U32, name="mc%d" % v, align_bytes=64)
+            msc[v] = keep.tile([P, Q], U8, name="msc%d" % v, align_bytes=64)
+        ss = keep.tile([P, 8], F32, name="ss")
+        rn = keep.tile([P, 8], F32, name="rn")
+        dot = keep.tile([P, 8], F32, name="dot")
+        sc = keep.tile([P, 8], F32, name="sc")
+        l0 = keep.tile([P, 8], F32, name="l0")
+        e0 = keep.tile([P, 8], F32, name="e0")
+        junk_v = keep.tile([P, D], F32, name="junk_v")
+
+        def view_codes(v):
+            tp = tps.tile([P, 2, 2, P], F32, name="tp")
+            for m in range(2):
+                words = xraw[v][:, m, :].bitcast(F32)
+                for u in range(2):
+                    nc.tensor.transpose(tp[:, m, u, :], words[:, u : D // 2 : 2], ident[:])
+            nc.scalar.copy(
+                out=gx[v][:].bitcast(F32).rearrange("p (m r u) -> p m r u", m=2, u=2),
+                in_=tp[:].rearrange("p m u r -> p m r u"),
+            )
+            nc.vector.quantize_mx(out=xc[v][:].bitcast(FP8X4), scales=xsc[v][:], in_=gx[v][:])
+
+        def row_dots_from_rows(i, j, dest, col):
+            for m in range(2):
+                nc.vector.scalar_tensor_tensor(
+                    out=junk_v[:], in0=xraw[i][:, m, :], scalar=1.0, in1=xraw[j][:, m, :], op0=ALU.mult, op1=ALU.mult,
+                    accum_out=dest[:, col + m : col + m + 1],
+                )
+
+        def row_dots_from_gram(i, j, dest, col):
+            gb = psum.tile([P, 2, P], F32, name="ps")
+            gi = gx[i][:].rearrange("p (c t) -> p c t", t=4)
+            gj = gx[j][:].rearrange("p (c t) -> p c t", t=4)
+            for m in range(2):
+                for t in range(4):
+                    nc.tensor.matmul(
+                        out=gb[:, m, :],
+                        lhsT=gi[:, P * m : P * (m + 1), t],
+                        rhs=gj[:, P * m : P * (m + 1), t],
+                        start=(t == 0),
+                        stop=(t == 3),
+                    )
+            for m in range(2):
+                nc.vector.scalar_tensor_tensor(
+                    out=junk_v[:, 0:P], in0=gb[:, m, :], scalar=1.0, in1=ident[:], op0=ALU.mult, op1=ALU.mult,
+                    accum_out=dest[:, col + m : col + m + 1],
+                )
+
+        def inverse_lengths(lo, hi):
+            nc.gpsimd.tensor_tensor(out=rn[:, lo:hi], in0=ss[:, lo:hi], in1=mhalf[:, 0 : hi - lo], op=ALU.pow)
+
+        def scale_of_pair(pi):
+            i, j = PAIRS[pi]
+            nc.vector.scalar_tensor_tensor(
+                out=sc[:, 2 * pi : 2 * pi + 2], in0=rn[:, 2 * i : 2 * i + 2], scalar=1.0 / TEMP,
+                in1=rn[:, 2 * j : 2 * j + 2], op0=ALU.mult, op1=ALU.mult,
+            )
+
+        def first_column(pi):
+            cols = slice(2 * pi, 2 * pi + 2)
+            nc.vector.tensor_tensor(out=l0[:, cols], in0=dot[:, cols], in1=sc[:, cols], op=ALU.mult)
+            nc.scalar.activation(out=e0[:, cols], in_=l0[:, cols], func=ACT.Exp)
+
+        def mem_turn(j, c, engines):
+            g = grp.tile([P, 4 * NT], BF16, name="g", align_bytes=64)
+            for h in range(2):
+                tp = tps.tile([P, 2, 2, P], F32, name="tp")
+                for a in range(2):
+                    words = mraw[(j, c)][:, 2 * h + a, :].bitcast(F32)
+                    for u in range(2):
+                        nc.tensor.transpose(tp[:, a, u, :], words[:, u : D // 2 : 2], ident[:])
+                dst = g[:, 1024 * h : 1024 * (h + 1)].bitcast(F32).rearrange("p (a r u) -> p a r u", a=2, u=2)
+                src = tp[:].rearrange("p a u r -> p a r u")
+                if engines[h] == "v":
+                    nc.vector.tensor_copy(out=dst, in_=src)
+                else:
+                    nc.scalar.copy(out=dst, in_=src)
+            return g
+
+        def mem_quantize(j, c, g):
+            cols = slice(NT * c, NT * (c + 1))
+            nc.vector.quantize_mx(out=mc[j][:, cols].bitcast(FP8X4), scales=msc[j][:, cols], in_=g[:])
+
+        row_dots_from_rows(1, 1, ss, 2)
+        row_dots_from_rows(0, 0, ss, 0)
+        view_codes(1)
+        inverse_lengths(0, 4)
+        scale_of_pair(0)
+        j0 = BANK_ORDER[0]
+        mem_quantize(j0, 0, mem_turn(j0, 0, ("s", "s")))
+        mem_quantize(j0, 1, mem_turn(j0, 1, ("s", "s")))
+        view_codes(2)
+        row_dots_from_gram(2, 2, ss, 4)
+        inverse_lengths(4, 6)
+        mem_quantize(j0, 2, mem_turn(j0, 2, ("s", "s")))
+        row_dots_from_rows(0, 1, dot, 0)
+        first_column(0)
+        mem_quantize(j0, 3, mem_turn(j0, 3, ("s", "s")))
+        scale_of_pair(1)
+        view_codes(0)
+        row_dots_from_gram(0, 2, dot, 2)
+        first_column(1)
+        view_codes(3)
+        row_dots_from_gram(3, 3, ss, 6)
+        inverse_lengths(6, 8)
+        scale_of_pair(2)
+        row_dots_from_gram(0, 3, dot, 4)
+        first_column(2)
+        scale_of_pair(3)
+        row_dots_from_gram(1, 2, dot, 6)
+        first_column(3)
+
+        units = []
+        for j in BANK_ORDER:
+            for ci in range(len(COMBOS)):
+                if COMBOS[ci][1] == j:
+                    units.append((ci, 0))
+                    units.append((ci, 1))
+        preps = []
+        for j in BANK_ORDER[1:]:
+            for c in range(4):
+                preps.append((j, c))
+        nu = len(units)
+        t_of = {}
+        am_of = {}
+        r4_of = {}
+        g_of = {}
+
+        def front(u):
+            ci, m = units[u]
+            i, j = COMBOS[ci]
+            col = 2 * PAIRS.index((min(i, j), max(i, j))) + m
+            rows = slice(P * m, P * (m + 1))
+            t = tpool.tile([P, W], F32, name="t")
+            t_of[u] = t
+            nc.gpsimd.tensor_copy(out=t[:, 0:1], in_=e0[:, col : col + 1])
+            for n in range(4):
+                cols = slice(NT * n, NT * (n + 1))
+                ps = psum.tile([P, NT], F32, name="ps")
+                nc.tensor.matmul_mx(
+                    out=ps[:],
+                    lhsT=xc[i][:, rows].bitcast(FP8X4),
+                    lhsT_scale=xsc[i][:, rows],
+                    rhs=mc[j][:, cols].bitcast(FP8X4),
+                    rhs_scale=msc[j][:, cols],
+                    start=True,
+                    stop=True,
+                )
+                nc.scalar.activation(
+                    out=t[:, 1 + NT * n : 1 + NT * (n + 1)], in_=ps[:], func=ACT.Exp, scale=sc[:, col : col + 1]
+                )
+                if u == nu - 1 and n == 1:
+                    nc.sync.dma_start(out=out_0[ci, rows, 0 : 1 + 2 * NT], in_=t[:, 0 : 1 + 2 * NT])
+            if u == nu - 1:
+                nc.sync.dma_start(out=out_0[ci, rows, 1 + 2 * NT : W], in_=t[:, 1 + 2 * NT : W])
+            else:
+                nc.sync.dma_start(out=out_0[ci, rows, :], in_=t[:])
+
+        def row_max(u):
+            am = small.tile([P, 1], F32, name="am")
+            am_of[u] = am
+            if u == nu - 1:
+                parts = small.tile([P, 4], F32, name="parts")
+                for n in range(4):
+                    lo = 0 if n == 0 else 1 + NT * n
+                    nc.vector.tensor_reduce(
+                        out=parts[:, n : n + 1], in_=t_of[u][:, lo : 1 + NT * (n + 1)], axis=AX.X, op=ALU.max
+                    )
+                nc.vector.tensor_reduce(out=am[:], in_=parts[:], axis=AX.X, op=ALU.max)
+            else:
+                nc.vector.tensor_reduce(out=am[:], in_=t_of[u][:], axis=AX.X, op=ALU.max)
+
+        def factor(u):
+            rc = small.tile([P, 1], F32, name="rc")
+            nc.vector.reciprocal(out=rc[:], in_=am_of[u][:])
+            r4 = small.tile([P, 1], F32, name="r4")
+            r4_of[u] = r4
+            nc.gpsimd.tensor_scalar(out=r4[:], in0=rc[:], scalar1=448.0, scalar2=1.0, op0=ALU.mult, op1=ALU.mult)
+
+        def cast(u):
+            ci, m = units[u]
+            rows = slice(P * m, P * (m + 1))
+            t = t_of[u]
+            r4 = r4_of[u]
+            cut = v_share(u, nu, len(preps))
+            o8 = opool.tile([P, W], FP8, name="o8")
+            if cut > 0:
+                nc.vector.tensor_scalar(
+                    out=o8[:, 0:cut], in0=t[:, 0:cut], scalar1=r4[:, 0:1], scalar2=None, op0=ALU.mult, saturate=False
+                )
+            nc.scalar.activation(
+                out=o8[:, cut:W], in_=t[:, cut:W], func=ACT.Identity, scale=r4[:, 0:1], bias=zero[:, 0:1],
+                saturate=False,
+            )
+            nc.sync.dma_start(out=out_1[ci, rows, :], in_=o8[:].bitcast(U8))
+
+        with tc.manual_schedule(engines={mybir.EngineType.DVE}):
+            for s in range(nu + 2):
+                if s < nu:
+                    front(s)
+                if s < len(preps):
+                    g_of[s] = mem_turn(preps[s][0], preps[s][1], ("s", "s"))
+                if 1 <= s <= nu:
+                    row_max(s - 1)
+                if s >= 2:
+                    cast(s - 2)
+                if 1 <= s <= nu:
+                    factor(s - 1)
+                if 1 <= s <= len(preps):
+                    mem_quantize(preps[s - 1][0], preps[s - 1][1], g_of[s - 1])

@@ -31,8 +31,8 @@ def v_share(u, n_units, n_preps):
     if u == n_units - 2:
         return 0
     if u + 2 < n_preps:
-        return 1728
-    return 1408
+        return 1664
+    return 1344
 
 
 def tile_memorymoco_pa_kernel(tc, x0, x1, x2, x3, mem0, mem1, mem2, mem3, out_0, out_1):
@@ -70,7 +70,7 @@ def tile_memorymoco_pa_kernel(tc, x0, x1, x2, x3, mem0, mem1, mem2, mem3, out_0,
         def load_chunk(j, c):
             mraw[(j, c)] = raw.tile([P, 4, D], BF16, name="mraw%d_%d" % (j, c))
             nc.sync.dma_start(
-                out=mraw[(j, c)][:], in_=mems[j][NT * c : NT * (c + 1), :].rearrange("(a p) k -> p a k", p=P)
+                out=mraw[(j, c)][:], in_=mems[j][NT * c : NT * (c + 1), :].rearrange("(p a) k -> p a k", p=P)
             )
 
         load_view(1)
@@ -116,14 +116,14 @@ def tile_memorymoco_pa_kernel(tc, x0, x1, x2, x3, mem0, mem1, mem2, mem3, out_0,
             )
             nc.vector.quantize_mx(out=xc[v][:].bitcast(FP8X4), scales=xsc[v][:], in_=gx[v][:])
 
-        def row_dots_from_rows(i, j, dest, col):
+        def row_dots_from_rows(i, j, dest, col, factor):
             for m in range(2):
                 nc.vector.scalar_tensor_tensor(
-                    out=junk_v[:], in0=xraw[i][:, m, :], scalar=1.0, in1=xraw[j][:, m, :], op0=ALU.mult, op1=ALU.mult,
+                    out=junk_v[:], in0=xraw[i][:, m, :], scalar=factor, in1=xraw[j][:, m, :], op0=ALU.mult, op1=ALU.mult,
                     accum_out=dest[:, col + m : col + m + 1],
                 )
 
-        def row_dots_from_gram(i, j, dest, col):
+        def row_dots_from_gram(i, j, dest, col, factor):
             gb = psum.tile([P, 2, P], F32, name="ps")
             gi = gx[i][:].rearrange("p (c t) -> p c t", t=4)
             gj = gx[j][:].rearrange("p (c t) -> p c t", t=4)
@@ -138,7 +138,7 @@ def tile_memorymoco_pa_kernel(tc, x0, x1, x2, x3, mem0, mem1, mem2, mem3, out_0,
                     )
             for m in range(2):
                 nc.vector.scalar_tensor_tensor(
-                    out=junk_v[:, 0:P], in0=gb[:, m, :], scalar=1.0, in1=ident[:], op0=ALU.mult, op1=ALU.mult,
+                    out=junk_v[:, 0:P], in0=gb[:, m, :], scalar=factor, in1=ident[:], op0=ALU.mult, op1=ALU.mult,
                     accum_out=dest[:, col + m : col + m + 1],
                 )
 
@@ -147,14 +147,13 @@ def tile_memorymoco_pa_kernel(tc, x0, x1, x2, x3, mem0, mem1, mem2, mem3, out_0,
 
         def scale_of_pair(pi):
             i, j = PAIRS[pi]
-            nc.vector.scalar_tensor_tensor(
-                out=sc[:, 2 * pi : 2 * pi + 2], in0=rn[:, 2 * i : 2 * i + 2], scalar=1.0 / TEMP,
-                in1=rn[:, 2 * j : 2 * j + 2], op0=ALU.mult, op1=ALU.mult,
+            nc.gpsimd.tensor_tensor(
+                out=sc[:, 2 * pi : 2 * pi + 2], in0=rn[:, 2 * i : 2 * i + 2], in1=rn[:, 2 * j : 2 * j + 2], op=ALU.mult
             )
 
         def first_column(pi):
             cols = slice(2 * pi, 2 * pi + 2)
-            nc.vector.tensor_tensor(out=l0[:, cols], in0=dot[:, cols], in1=sc[:, cols], op=ALU.mult)
+            nc.gpsimd.tensor_tensor(out=l0[:, cols], in0=dot[:, cols], in1=sc[:, cols], op=ALU.mult)
             nc.scalar.activation(out=e0[:, cols], in_=l0[:, cols], func=ACT.Exp)
 
         def mem_turn(j, c, engines):
@@ -177,33 +176,33 @@ def tile_memorymoco_pa_kernel(tc, x0, x1, x2, x3, mem0, mem1, mem2, mem3, out_0,
             cols = slice(NT * c, NT * (c + 1))
             nc.vector.quantize_mx(out=mc[j][:, cols].bitcast(FP8X4), scales=msc[j][:, cols], in_=g[:])
 
-        row_dots_from_rows(1, 1, ss, 2)
-        row_dots_from_rows(0, 0, ss, 0)
+        j0 = BANK_ORDER[0]
+        row_dots_from_rows(1, 1, ss, 2, TEMP)
+        row_dots_from_rows(0, 0, ss, 0, TEMP)
         view_codes(1)
+        view_codes(0)
         inverse_lengths(0, 4)
         scale_of_pair(0)
-        j0 = BANK_ORDER[0]
         mem_quantize(j0, 0, mem_turn(j0, 0, ("s", "s")))
         mem_quantize(j0, 1, mem_turn(j0, 1, ("s", "s")))
+        row_dots_from_gram(0, 1, dot, 0, 1.0)
+        first_column(0)
         view_codes(2)
-        row_dots_from_gram(2, 2, ss, 4)
+        row_dots_from_gram(2, 2, ss, 4, TEMP)
         inverse_lengths(4, 6)
         mem_quantize(j0, 2, mem_turn(j0, 2, ("s", "s")))
-        row_dots_from_rows(0, 1, dot, 0)
-        first_column(0)
         mem_quantize(j0, 3, mem_turn(j0, 3, ("s", "s")))
         scale_of_pair(1)
-        view_codes(0)
-        row_dots_from_gram(0, 2, dot, 2)
+        row_dots_from_gram(0, 2, dot, 2, 1.0)
         first_column(1)
         view_codes(3)
-        row_dots_from_gram(3, 3, ss, 6)
+        row_dots_from_gram(3, 3, ss, 6, TEMP)
         inverse_lengths(6, 8)
         scale_of_pair(2)
-        row_dots_from_gram(0, 3, dot, 4)
+        row_dots_from_gram(0, 3, dot, 4, 1.0)
         first_column(2)
         scale_of_pair(3)
-        row_dots_from_gram(1, 2, dot, 6)
+        row_dots_from_gram(1, 2, dot, 6, 1.0)
         first_column(3)
 
         units = []
@@ -243,7 +242,10 @@ def tile_memorymoco_pa_kernel(tc, x0, x1, x2, x3, mem0, mem1, mem2, mem3, out_0,
                     stop=True,
                 )
                 nc.scalar.activation(
-                    out=t[:, 1 + NT * n : 1 + NT * (n + 1)], in_=ps[:], func=ACT.Exp, scale=sc[:, col : col + 1]
+                    out=t[:, 1 + NT * n : 1 + NT * (n + 1)].rearrange("p (r a) -> p r a", a=4),
+                    in_=ps[:].rearrange("p (a r) -> p r a", a=4),
+                    func=ACT.Exp,
+                    scale=sc[:, col : col + 1],
                 )
                 if u == nu - 1 and n == 1:
                     nc.sync.dma_start(out=out_0[ci, rows, 0 : 1 + 2 * NT], in_=t[:, 0 : 1 + 2 * NT])

@@ -31,7 +31,9 @@ def v_share(u, n_units, n_preps):
     if u == n_units - 2:
         return 0
     if u + 2 < n_preps:
-        return 1664
+        return 1408 if u % 2 == 0 else W
+    if u + 2 == n_preps:
+        return 704
     return 1344
 
 
@@ -45,6 +47,7 @@ def tile_memorymoco_pa_kernel(tc, x0, x1, x2, x3, mem0, mem1, mem2, mem3, out_0,
         raw = ctx.enter_context(tc.tile_pool(name="raw", bufs=1))
         keep = ctx.enter_context(tc.tile_pool(name="keep", bufs=1))
         grp = ctx.enter_context(tc.tile_pool(name="grp", bufs=3))
+        grp2 = ctx.enter_context(tc.tile_pool(name="grp2", bufs=2))
         tpool = ctx.enter_context(tc.tile_pool(name="tpool", bufs=6))
         opool = ctx.enter_context(tc.tile_pool(name="opool", bufs=4))
         small = ctx.enter_context(tc.tile_pool(name="small", bufs=4))
@@ -156,25 +159,25 @@ def tile_memorymoco_pa_kernel(tc, x0, x1, x2, x3, mem0, mem1, mem2, mem3, out_0,
             nc.gpsimd.tensor_tensor(out=l0[:, cols], in0=dot[:, cols], in1=sc[:, cols], op=ALU.mult)
             nc.scalar.activation(out=e0[:, cols], in_=l0[:, cols], func=ACT.Exp)
 
-        def mem_turn(j, c, engines):
-            g = grp.tile([P, 4 * NT], BF16, name="g", align_bytes=64)
+        def mem_turn(j, c, g, base):
             for h in range(2):
                 tp = tps.tile([P, 2, 2, P], F32, name="tp")
                 for a in range(2):
                     words = mraw[(j, c)][:, 2 * h + a, :].bitcast(F32)
                     for u in range(2):
                         nc.tensor.transpose(tp[:, a, u, :], words[:, u : D // 2 : 2], ident[:])
-                dst = g[:, 1024 * h : 1024 * (h + 1)].bitcast(F32).rearrange("p (a r u) -> p a r u", a=2, u=2)
-                src = tp[:].rearrange("p a u r -> p a r u")
-                if engines[h] == "v":
-                    nc.vector.tensor_copy(out=dst, in_=src)
-                else:
-                    nc.scalar.copy(out=dst, in_=src)
-            return g
+                lo = base + 1024 * h
+                dst = g[:, lo : lo + 1024].bitcast(F32).rearrange("p (a r u) -> p a r u", a=2, u=2)
+                nc.scalar.copy(out=dst, in_=tp[:].rearrange("p a u r -> p a r u"))
 
-        def mem_quantize(j, c, g):
-            cols = slice(NT * c, NT * (c + 1))
+        def mem_quantize(j, c, n_chunks, g):
+            cols = slice(NT * c, NT * (c + n_chunks))
             nc.vector.quantize_mx(out=mc[j][:, cols].bitcast(FP8X4), scales=msc[j][:, cols], in_=g[:])
+
+        def head_chunk(j, c):
+            g = grp.tile([P, 4 * NT], BF16, name="g", align_bytes=64)
+            mem_turn(j, c, g, 0)
+            mem_quantize(j, c, 1, g)
 
         j0 = BANK_ORDER[0]
         row_dots_from_rows(1, 1, ss, 2, TEMP)
@@ -183,15 +186,15 @@ def tile_memorymoco_pa_kernel(tc, x0, x1, x2, x3, mem0, mem1, mem2, mem3, out_0,
         view_codes(0)
         inverse_lengths(0, 4)
         scale_of_pair(0)
-        mem_quantize(j0, 0, mem_turn(j0, 0, ("s", "s")))
-        mem_quantize(j0, 1, mem_turn(j0, 1, ("s", "s")))
+        head_chunk(j0, 0)
+        head_chunk(j0, 1)
         row_dots_from_gram(0, 1, dot, 0, 1.0)
         first_column(0)
         view_codes(2)
         row_dots_from_gram(2, 2, ss, 4, TEMP)
         inverse_lengths(4, 6)
-        mem_quantize(j0, 2, mem_turn(j0, 2, ("s", "s")))
-        mem_quantize(j0, 3, mem_turn(j0, 3, ("s", "s")))
+        head_chunk(j0, 2)
+        head_chunk(j0, 3)
         scale_of_pair(1)
         row_dots_from_gram(0, 2, dot, 2, 1.0)
         first_column(1)
@@ -286,10 +289,11 @@ def tile_memorymoco_pa_kernel(tc, x0, x1, x2, x3, mem0, mem1, mem2, mem3, out_0,
                 nc.vector.tensor_scalar(
                     out=o8[:, 0:cut], in0=t[:, 0:cut], scalar1=r4[:, 0:1], scalar2=None, op0=ALU.mult, saturate=False
                 )
-            nc.scalar.activation(
-                out=o8[:, cut:W], in_=t[:, cut:W], func=ACT.Identity, scale=r4[:, 0:1], bias=zero[:, 0:1],
-                saturate=False,
-            )
+            if cut < W:
+                nc.scalar.activation(
+                    out=o8[:, cut:W], in_=t[:, cut:W], func=ACT.Identity, scale=r4[:, 0:1], bias=zero[:, 0:1],
+                    saturate=False,
+                )
             nc.sync.dma_start(out=out_1[ci, rows, :], in_=o8[:].bitcast(U8))
 
         with tc.manual_schedule(engines={mybir.EngineType.DVE}):
@@ -297,12 +301,14 @@ def tile_memorymoco_pa_kernel(tc, x0, x1, x2, x3, mem0, mem1, mem2, mem3, out_0,
                 if s < nu:
                     front(s)
                 if s < len(preps):
-                    g_of[s] = mem_turn(preps[s][0], preps[s][1], ("s", "s"))
+                    if s % 2 == 0:
+                        g_of[s // 2] = grp2.tile([P, 8 * NT], BF16, name="g2", align_bytes=64)
+                    mem_turn(preps[s][0], preps[s][1], g_of[s // 2], 4 * NT * (s % 2))
                 if 1 <= s <= nu:
                     row_max(s - 1)
                 if s >= 2:
                     cast(s - 2)
                 if 1 <= s <= nu:
                     factor(s - 1)
-                if 1 <= s <= len(preps):
-                    mem_quantize(preps[s - 1][0], preps[s - 1][1], g_of[s - 1])
+                if 2 <= s <= len(preps) and s % 2 == 0:
+                    mem_quantize(preps[s - 2][0], preps[s - 2][1], 2, g_of[s // 2 - 1])

@@ -25,18 +25,6 @@ PAIRS = ((0, 1), (0, 2), (0, 3), (1, 2))
 BANK_ORDER = (0, 1, 2, 3)
 
 
-def v_share(u, n_units, n_preps):
-    if u == n_units - 1:
-        return 1344
-    if u == n_units - 2:
-        return 0
-    if u + 2 < n_preps:
-        return 1408 if u % 2 == 0 else W
-    if u + 2 == n_preps:
-        return 704
-    return 1344
-
-
 def tile_memorymoco_pa_kernel(tc, x0, x1, x2, x3, mem0, mem1, mem2, mem3, out_0, out_1):
     nc = tc.nc
     xs = (x0, x1, x2, x3)
@@ -47,12 +35,11 @@ def tile_memorymoco_pa_kernel(tc, x0, x1, x2, x3, mem0, mem1, mem2, mem3, out_0,
         raw = ctx.enter_context(tc.tile_pool(name="raw", bufs=1))
         keep = ctx.enter_context(tc.tile_pool(name="keep", bufs=1))
         grp = ctx.enter_context(tc.tile_pool(name="grp", bufs=3))
-        grp2 = ctx.enter_context(tc.tile_pool(name="grp2", bufs=2))
         tpool = ctx.enter_context(tc.tile_pool(name="tpool", bufs=6))
         opool = ctx.enter_context(tc.tile_pool(name="opool", bufs=4))
         small = ctx.enter_context(tc.tile_pool(name="small", bufs=4))
-        tps = ctx.enter_context(tc.psum_pool(name="tps", bufs=2))
-        psum = ctx.enter_context(tc.psum_pool(name="psum", bufs=6))
+        tps = ctx.enter_context(tc.psum_pool(name="tps", bufs=3))
+        psum = ctx.enter_context(tc.psum_pool(name="psum", bufs=5))
 
         ident = const.tile([P, P], F32, name="ident")
         make_identity(nc, ident[:])
@@ -62,6 +49,8 @@ def tile_memorymoco_pa_kernel(tc, x0, x1, x2, x3, mem0, mem1, mem2, mem3, out_0,
         nc.vector.memset(zero[:], 0.0)
         warm = const.tile([P, 1], F32, name="warm")
         nc.scalar.activation(out=warm[:], in_=zero[:], func=ACT.Exp)
+
+        ctx.enter_context(tc.manual_schedule())
 
         xraw = {}
         mraw = {}
@@ -77,13 +66,13 @@ def tile_memorymoco_pa_kernel(tc, x0, x1, x2, x3, mem0, mem1, mem2, mem3, out_0,
             )
 
         load_view(1)
+        load_chunk(0, 0)
         load_view(0)
-        load_chunk(BANK_ORDER[0], 0)
-        load_chunk(BANK_ORDER[0], 1)
+        load_chunk(0, 1)
         load_view(2)
+        load_chunk(0, 2)
+        load_chunk(0, 3)
         load_view(3)
-        load_chunk(BANK_ORDER[0], 2)
-        load_chunk(BANK_ORDER[0], 3)
         for j in BANK_ORDER[1:]:
             for c in range(4):
                 load_chunk(j, c)
@@ -105,29 +94,70 @@ def tile_memorymoco_pa_kernel(tc, x0, x1, x2, x3, mem0, mem1, mem2, mem3, out_0,
         sc = keep.tile([P, 8], F32, name="sc")
         l0 = keep.tile([P, 8], F32, name="l0")
         e0 = keep.tile([P, 8], F32, name="e0")
-        junk_v = keep.tile([P, D], F32, name="junk_v")
+        i0 = keep.tile([P, 8], F32, name="i0")
+        r0 = keep.tile([P, 8], F32, name="r0")
+        junks = [keep.tile([P, D], F32, name="junk%d" % m) for m in range(2)]
 
-        def view_codes(v):
+
+        tp_of = {}
+
+        def turn_view(v):
             tp = tps.tile([P, 2, 2, P], F32, name="tp")
+            tp_of[("x", v)] = tp
             for m in range(2):
                 words = xraw[v][:, m, :].bitcast(F32)
                 for u in range(2):
                     nc.tensor.transpose(tp[:, m, u, :], words[:, u : D // 2 : 2], ident[:])
-            nc.scalar.copy(
+
+        def move_view(v, copy):
+            copy(
                 out=gx[v][:].bitcast(F32).rearrange("p (m r u) -> p m r u", m=2, u=2),
-                in_=tp[:].rearrange("p m u r -> p m r u"),
+                in_=tp_of[("x", v)][:].rearrange("p m u r -> p m r u"),
             )
+
+        def quantize_view(v):
             nc.vector.quantize_mx(out=xc[v][:].bitcast(FP8X4), scales=xsc[v][:], in_=gx[v][:])
 
-        def row_dots_from_rows(i, j, dest, col, factor):
-            for m in range(2):
+        g_of = {}
+
+        def turn_half(j, c, h):
+            tp = tps.tile([P, 2, 2, P], F32, name="tp")
+            tp_of[(j, c, h)] = tp
+            for a in range(2):
+                words = mraw[(j, c)][:, 2 * h + a, :].bitcast(F32)
+                for u in range(2):
+                    nc.tensor.transpose(tp[:, a, u, :], words[:, u : D // 2 : 2], ident[:])
+
+        def move_half(j, c, h, copy):
+            if h == 0:
+                g_of[(j, c)] = grp.tile([P, 4 * NT], BF16, name="g", align_bytes=64)
+            lo = 1024 * h
+            dst = g_of[(j, c)][:, lo : lo + 1024].bitcast(F32).rearrange("p (a r u) -> p a r u", a=2, u=2)
+            copy(out=dst, in_=tp_of[(j, c, h)][:].rearrange("p a u r -> p a r u"))
+
+        def quantize_chunk(j, c):
+            cols = slice(NT * c, NT * (c + 1))
+            nc.vector.quantize_mx(out=mc[j][:, cols].bitcast(FP8X4), scales=msc[j][:, cols], in_=g_of[(j, c)][:])
+
+        def squares_from_rows(v, halves=(0, 1)):
+            for m in halves:
                 nc.vector.scalar_tensor_tensor(
-                    out=junk_v[:], in0=xraw[i][:, m, :], scalar=factor, in1=xraw[j][:, m, :], op0=ALU.mult, op1=ALU.mult,
-                    accum_out=dest[:, col + m : col + m + 1],
+                    out=junks[m][:], in0=xraw[v][:, m, :], scalar=TEMP, in1=xraw[v][:, m, :], op0=ALU.mult, op1=ALU.mult,
+                    accum_out=ss[:, 2 * v + m : 2 * v + m + 1],
                 )
 
-        def row_dots_from_gram(i, j, dest, col, factor):
+        def dots_from_rows(i, j, pi, halves=(0, 1)):
+            for m in halves:
+                nc.vector.scalar_tensor_tensor(
+                    out=junks[m][:], in0=xraw[i][:, m, :], scalar=1.0, in1=xraw[j][:, m, :], op0=ALU.mult, op1=ALU.mult,
+                    accum_out=dot[:, 2 * pi + m : 2 * pi + m + 1],
+                )
+
+        gb_of = {}
+
+        def gram(i, j):
             gb = psum.tile([P, 2, P], F32, name="ps")
+            gb_of[(i, j)] = gb
             gi = gx[i][:].rearrange("p (c t) -> p c t", t=4)
             gj = gx[j][:].rearrange("p (c t) -> p c t", t=4)
             for m in range(2):
@@ -139,14 +169,17 @@ def tile_memorymoco_pa_kernel(tc, x0, x1, x2, x3, mem0, mem1, mem2, mem3, out_0,
                         start=(t == 0),
                         stop=(t == 3),
                     )
+
+        def pick(i, j, dest, col, factor):
             for m in range(2):
                 nc.vector.scalar_tensor_tensor(
-                    out=junk_v[:, 0:P], in0=gb[:, m, :], scalar=factor, in1=ident[:], op0=ALU.mult, op1=ALU.mult,
+                    out=junks[m][:, 0:P], in0=gb_of[(i, j)][:, m, :], scalar=factor, in1=ident[:], op0=ALU.mult, op1=ALU.mult,
                     accum_out=dest[:, col + m : col + m + 1],
                 )
 
-        def inverse_lengths(lo, hi):
-            nc.gpsimd.tensor_tensor(out=rn[:, lo:hi], in0=ss[:, lo:hi], in1=mhalf[:, 0 : hi - lo], op=ALU.pow)
+        def inverse_lengths(v):
+            cols = slice(2 * v, 2 * v + 2)
+            nc.gpsimd.tensor_tensor(out=rn[:, cols], in0=ss[:, cols], in1=mhalf[:, 0:2], op=ALU.pow)
 
         def scale_of_pair(pi):
             i, j = PAIRS[pi]
@@ -154,161 +187,299 @@ def tile_memorymoco_pa_kernel(tc, x0, x1, x2, x3, mem0, mem1, mem2, mem3, out_0,
                 out=sc[:, 2 * pi : 2 * pi + 2], in0=rn[:, 2 * i : 2 * i + 2], in1=rn[:, 2 * j : 2 * j + 2], op=ALU.mult
             )
 
-        def first_column(pi):
+        def first_logit(pi):
             cols = slice(2 * pi, 2 * pi + 2)
             nc.gpsimd.tensor_tensor(out=l0[:, cols], in0=dot[:, cols], in1=sc[:, cols], op=ALU.mult)
+
+        def first_exp(pi):
+            cols = slice(2 * pi, 2 * pi + 2)
             nc.scalar.activation(out=e0[:, cols], in_=l0[:, cols], func=ACT.Exp)
 
-        def mem_turn(j, c, g, base):
-            for h in range(2):
-                tp = tps.tile([P, 2, 2, P], F32, name="tp")
-                for a in range(2):
-                    words = mraw[(j, c)][:, 2 * h + a, :].bitcast(F32)
-                    for u in range(2):
-                        nc.tensor.transpose(tp[:, a, u, :], words[:, u : D // 2 : 2], ident[:])
-                lo = base + 1024 * h
-                dst = g[:, lo : lo + 1024].bitcast(F32).rearrange("p (a r u) -> p a r u", a=2, u=2)
-                nc.scalar.copy(out=dst, in_=tp[:].rearrange("p a u r -> p a r u"))
-
-        def mem_quantize(j, c, n_chunks, g):
-            cols = slice(NT * c, NT * (c + n_chunks))
-            nc.vector.quantize_mx(out=mc[j][:, cols].bitcast(FP8X4), scales=msc[j][:, cols], in_=g[:])
-
-        def head_chunk(j, c):
-            g = grp.tile([P, 4 * NT], BF16, name="g", align_bytes=64)
-            mem_turn(j, c, g, 0)
-            mem_quantize(j, c, 1, g)
-
-        j0 = BANK_ORDER[0]
-        row_dots_from_rows(1, 1, ss, 2, TEMP)
-        row_dots_from_rows(0, 0, ss, 0, TEMP)
-        view_codes(1)
-        view_codes(0)
-        inverse_lengths(0, 4)
-        scale_of_pair(0)
-        head_chunk(j0, 0)
-        head_chunk(j0, 1)
-        row_dots_from_gram(0, 1, dot, 0, 1.0)
-        first_column(0)
-        view_codes(2)
-        row_dots_from_gram(2, 2, ss, 4, TEMP)
-        inverse_lengths(4, 6)
-        head_chunk(j0, 2)
-        head_chunk(j0, 3)
-        scale_of_pair(1)
-        row_dots_from_gram(0, 2, dot, 2, 1.0)
-        first_column(1)
-        view_codes(3)
-        row_dots_from_gram(3, 3, ss, 6, TEMP)
-        inverse_lengths(6, 8)
-        scale_of_pair(2)
-        row_dots_from_gram(0, 3, dot, 4, 1.0)
-        first_column(2)
-        scale_of_pair(3)
-        row_dots_from_gram(1, 2, dot, 6, 1.0)
-        first_column(3)
+        def first_factor(pi):
+            cols = slice(2 * pi, 2 * pi + 2)
+            nc.vector.reciprocal(out=i0[:, cols], in_=e0[:, cols])
+            nc.gpsimd.tensor_scalar(out=r0[:, cols], in0=i0[:, cols], scalar1=448.0, scalar2=1.0, op0=ALU.mult, op1=ALU.mult)
 
         units = []
-        for j in BANK_ORDER:
+        for j in range(4):
             for ci in range(len(COMBOS)):
                 if COMBOS[ci][1] == j:
                     units.append((ci, 0))
                     units.append((ci, 1))
-        preps = []
-        for j in BANK_ORDER[1:]:
-            for c in range(4):
-                preps.append((j, c))
         nu = len(units)
         t_of = {}
         am_of = {}
         r4_of = {}
-        g_of = {}
+        rc_of = {}
+        ps_of = {}
+        parts_of = {}
 
-        def front(u):
+        def pair_col(u):
             ci, m = units[u]
             i, j = COMBOS[ci]
-            col = 2 * PAIRS.index((min(i, j), max(i, j))) + m
+            return 2 * PAIRS.index((min(i, j), max(i, j))) + m
+
+        def product(u, n):
+            if u >= nu:
+                return
+            ci, m = units[u]
+            i, j = COMBOS[ci]
             rows = slice(P * m, P * (m + 1))
-            t = tpool.tile([P, W], F32, name="t")
-            t_of[u] = t
-            nc.gpsimd.tensor_copy(out=t[:, 0:1], in_=e0[:, col : col + 1])
-            for n in range(4):
-                cols = slice(NT * n, NT * (n + 1))
-                ps = psum.tile([P, NT], F32, name="ps")
-                nc.tensor.matmul_mx(
-                    out=ps[:],
-                    lhsT=xc[i][:, rows].bitcast(FP8X4),
-                    lhsT_scale=xsc[i][:, rows],
-                    rhs=mc[j][:, cols].bitcast(FP8X4),
-                    rhs_scale=msc[j][:, cols],
-                    start=True,
-                    stop=True,
-                )
-                nc.scalar.activation(
-                    out=t[:, 1 + NT * n : 1 + NT * (n + 1)].rearrange("p (r a) -> p r a", a=4),
-                    in_=ps[:].rearrange("p (a r) -> p r a", a=4),
-                    func=ACT.Exp,
-                    scale=sc[:, col : col + 1],
-                )
-                if u == nu - 1 and n == 1:
-                    nc.sync.dma_start(out=out_0[ci, rows, 0 : 1 + 2 * NT], in_=t[:, 0 : 1 + 2 * NT])
-            if u == nu - 1:
-                nc.sync.dma_start(out=out_0[ci, rows, 1 + 2 * NT : W], in_=t[:, 1 + 2 * NT : W])
-            else:
-                nc.sync.dma_start(out=out_0[ci, rows, :], in_=t[:])
+            cols = slice(NT * n, NT * (n + 1))
+            ps = psum.tile([P, NT], F32, name="ps")
+            ps_of[(u, n)] = ps
+            nc.tensor.matmul_mx(
+                out=ps[:],
+                lhsT=xc[i][:, rows].bitcast(FP8X4),
+                lhsT_scale=xsc[i][:, rows],
+                rhs=mc[j][:, cols].bitcast(FP8X4),
+                rhs_scale=msc[j][:, cols],
+                start=True,
+                stop=True,
+            )
+
+        def exp_chunk(u, n):
+            if n == 0:
+                t_of[u] = tpool.tile([P, W], F32, name="t")
+            col = pair_col(u)
+            nc.scalar.activation(
+                out=t_of[u][:, 1 + NT * n : 1 + NT * (n + 1)].rearrange("p (r a) -> p r a", a=4),
+                in_=ps_of[(u, n)][:].rearrange("p (a r) -> p r a", a=4),
+                func=ACT.Exp,
+                scale=sc[:, col : col + 1],
+            )
+
+        def column_zero(u):
+            col = pair_col(u)
+            nc.gpsimd.tensor_copy(out=t_of[u][:, 0:1], in_=e0[:, col : col + 1])
+
+        def store(u, lo, hi):
+            ci, m = units[u]
+            nc.sync.dma_start(out=out_0[ci, P * m : P * (m + 1), lo:hi], in_=t_of[u][:, lo:hi])
+
+        def part_max(u, n):
+            if u not in parts_of:
+                parts_of[u] = small.tile([P, 4], F32, name="parts")
+            nc.vector.tensor_reduce(
+                out=parts_of[u][:, n : n + 1], in_=t_of[u][:, 1 + NT * n : 1 + NT * (n + 1)], axis=AX.X, op=ALU.max
+            )
+
+        def fold_max(u):
+            am_of[u] = small.tile([P, 1], F32, name="am")
+            nc.vector.tensor_reduce(out=am_of[u][:], in_=parts_of[u][:], axis=AX.X, op=ALU.max)
 
         def row_max(u):
-            am = small.tile([P, 1], F32, name="am")
-            am_of[u] = am
-            if u == nu - 1:
-                parts = small.tile([P, 4], F32, name="parts")
-                for n in range(4):
-                    lo = 0 if n == 0 else 1 + NT * n
-                    nc.vector.tensor_reduce(
-                        out=parts[:, n : n + 1], in_=t_of[u][:, lo : 1 + NT * (n + 1)], axis=AX.X, op=ALU.max
-                    )
-                nc.vector.tensor_reduce(out=am[:], in_=parts[:], axis=AX.X, op=ALU.max)
-            else:
-                nc.vector.tensor_reduce(out=am[:], in_=t_of[u][:], axis=AX.X, op=ALU.max)
+            am_of[u] = small.tile([P, 1], F32, name="am")
+            nc.vector.tensor_reduce(out=am_of[u][:], in_=t_of[u][:, 1:W], axis=AX.X, op=ALU.max)
 
         def factor(u):
+            col = pair_col(u)
             rc = small.tile([P, 1], F32, name="rc")
             nc.vector.reciprocal(out=rc[:], in_=am_of[u][:])
             r4 = small.tile([P, 1], F32, name="r4")
             r4_of[u] = r4
-            nc.gpsimd.tensor_scalar(out=r4[:], in0=rc[:], scalar1=448.0, scalar2=1.0, op0=ALU.mult, op1=ALU.mult)
+            nc.gpsimd.tensor_scalar(out=r4[:], in0=rc[:], scalar1=448.0, scalar2=r0[:, col : col + 1], op0=ALU.mult, op1=ALU.min)
 
-        def cast(u):
-            ci, m = units[u]
-            rows = slice(P * m, P * (m + 1))
-            t = t_of[u]
-            r4 = r4_of[u]
-            cut = v_share(u, nu, len(preps))
-            o8 = opool.tile([P, W], FP8, name="o8")
+        o8_of = {}
+
+        def cast_v(u, cut):
+            o8_of[u] = opool.tile([P, W], FP8, name="o8")
             if cut > 0:
                 nc.vector.tensor_scalar(
-                    out=o8[:, 0:cut], in0=t[:, 0:cut], scalar1=r4[:, 0:1], scalar2=None, op0=ALU.mult, saturate=False
-                )
-            if cut < W:
-                nc.scalar.activation(
-                    out=o8[:, cut:W], in_=t[:, cut:W], func=ACT.Identity, scale=r4[:, 0:1], bias=zero[:, 0:1],
+                    out=o8_of[u][:, 0:cut], in0=t_of[u][:, 0:cut], scalar1=r4_of[u][:, 0:1], scalar2=None, op0=ALU.mult,
                     saturate=False,
                 )
-            nc.sync.dma_start(out=out_1[ci, rows, :], in_=o8[:].bitcast(U8))
 
-        with tc.manual_schedule(engines={mybir.EngineType.DVE}):
-            for s in range(nu + 2):
-                if s < nu:
-                    front(s)
-                if s < len(preps):
-                    if s % 2 == 0:
-                        g_of[s // 2] = grp2.tile([P, 8 * NT], BF16, name="g2", align_bytes=64)
-                    mem_turn(preps[s][0], preps[s][1], g_of[s // 2], 4 * NT * (s % 2))
-                if 1 <= s <= nu:
-                    row_max(s - 1)
-                if s >= 2:
-                    cast(s - 2)
-                if 1 <= s <= nu:
-                    factor(s - 1)
-                if 2 <= s <= len(preps) and s % 2 == 0:
-                    mem_quantize(preps[s - 2][0], preps[s - 2][1], 2, g_of[s // 2 - 1])
+        def cast_s(u, cut):
+            if cut < W:
+                nc.scalar.activation(
+                    out=o8_of[u][:, cut:W], in_=t_of[u][:, cut:W], func=ACT.Identity, scale=r4_of[u][:, 0:1],
+                    bias=zero[:, 0:1], saturate=False,
+                )
+
+        def store_bytes(u):
+            ci, m = units[u]
+            nc.sync.dma_start(out=out_1[ci, P * m : P * (m + 1), :], in_=o8_of[u][:].bitcast(U8))
+
+        sca = nc.scalar.copy
+        vec = nc.vector.tensor_copy
+
+        turn_view(1)
+        turn_half(0, 0, 0)
+        turn_half(0, 0, 1)
+        squares_from_rows(1)
+        inverse_lengths(1)
+        move_view(1, sca)
+        squares_from_rows(0, (0,))
+        quantize_view(1)
+        squares_from_rows(0, (1,))
+        inverse_lengths(0)
+        scale_of_pair(0)
+        move_half(0, 0, 0, sca)
+        move_half(0, 0, 1, sca)
+        turn_half(0, 1, 0)
+        turn_half(0, 1, 1)
+        dots_from_rows(0, 1, 0, (0,))
+        quantize_chunk(0, 0)
+        dots_from_rows(0, 1, 0, (1,))
+        first_logit(0)
+        move_half(0, 1, 0, sca)
+        move_half(0, 1, 1, sca)
+        turn_view(2)
+        product(0, 0)
+        product(1, 0)
+        squares_from_rows(2, (0,))
+        quantize_chunk(0, 1)
+        turn_half(0, 2, 0)
+        turn_half(0, 2, 1)
+        exp_chunk(0, 0)
+        exp_chunk(1, 0)
+        product(0, 1)
+        product(1, 1)
+        move_view(2, vec)
+        squares_from_rows(2, (1,))
+        inverse_lengths(2)
+        scale_of_pair(1)
+        quantize_view(2)
+        move_half(0, 2, 0, sca)
+        move_half(0, 2, 1, sca)
+        quantize_chunk(0, 2)
+        turn_half(0, 3, 0)
+        turn_half(0, 3, 1)
+        turn_view(3)
+        exp_chunk(0, 1)
+        exp_chunk(1, 1)
+        first_exp(0)
+        column_zero(0)
+        column_zero(1)
+        product(0, 2)
+        product(1, 2)
+        product(2, 0)
+        part_max(0, 0)
+        part_max(1, 0)
+        move_half(0, 3, 0, sca)
+        move_half(0, 3, 1, sca)
+        turn_view(0)
+        part_max(0, 1)
+        part_max(1, 1)
+        quantize_chunk(0, 3)
+        exp_chunk(0, 2)
+        exp_chunk(1, 2)
+        product(2, 1)
+        turn_half(1, 0, 0)
+        product(0, 3)
+        product(1, 3)
+        exp_chunk(2, 0)
+        exp_chunk(2, 1)
+        move_view(3, vec)
+        move_view(0, vec)
+        turn_half(1, 0, 1)
+        product(2, 2)
+        product(2, 3)
+        quantize_view(3)
+        quantize_view(0)
+        first_factor(0)
+        part_max(0, 2)
+        part_max(1, 2)
+        move_half(1, 0, 0, sca)
+        exp_chunk(0, 3)
+        exp_chunk(1, 3)
+        store(0, 0, W)
+        store(1, 0, W)
+        part_max(0, 3)
+        part_max(1, 3)
+        fold_max(0)
+        fold_max(1)
+        factor(0)
+        factor(1)
+        gram(0, 2)
+        gram(3, 3)
+        exp_chunk(2, 2)
+        exp_chunk(2, 3)
+        move_half(1, 0, 1, sca)
+        product(3, 0)
+        turn_half(1, 1, 0)
+        turn_half(1, 1, 1)
+        cast_v(0, 1600)
+        cast_s(0, 1600)
+        store_bytes(0)
+        pick(3, 3, ss, 6, TEMP)
+        pick(0, 2, dot, 2, 1.0)
+        first_logit(1)
+        inverse_lengths(3)
+        scale_of_pair(2)
+        quantize_chunk(1, 0)
+        product(3, 1)
+        product(3, 2)
+        product(3, 3)
+
+        preps = [(j, c) for j in (1, 2, 3) for c in range(4)]
+        LEAD = 4
+
+        def prep_of(s):
+            return preps[s - 2] if 2 <= s < 2 + len(preps) else None
+
+        def cut_of(u):
+            if u == nu - 1:
+                return 1344
+            if u == nu - 2:
+                return 0
+            return 1600 if prep_of(u + 2) else 1280
+
+        def ahead(s, n):
+            k = 4 * s + n + LEAD
+            product(k // 4, k % 4)
+
+        for s in range(3, nu + 2):
+            prep = prep_of(s)
+            follow = prep_of(s + 1)
+            if prep:
+                move_half(prep[0], prep[1], 0, sca)
+                move_half(prep[0], prep[1], 1, sca)
+            if follow:
+                turn_half(follow[0], follow[1], 0)
+                turn_half(follow[0], follow[1], 1)
+            if s < nu:
+                row_max(s - 1)
+            elif s == nu:
+                for n in range(4):
+                    part_max(s - 1, n)
+                fold_max(s - 1)
+            if prep:
+                quantize_chunk(*prep)
+            if s < nu:
+                for n in range(4):
+                    exp_chunk(s, n)
+                    ahead(s, n)
+                    if n == 1 and s == 3:
+                        first_exp(1)
+                        column_zero(2)
+                        store(2, 0, W)
+                        column_zero(3)
+                        gram(0, 3)
+                        gram(1, 2)
+                    if n == 1 and s == nu - 1:
+                        column_zero(s)
+                        store(s, 0, 1 + 2 * NT)
+                if 4 < s < nu - 1:
+                    column_zero(s)
+                if s == 4:
+                    first_exp(2)
+                    first_exp(3)
+                    column_zero(4)
+                store(s, 0 if s < nu - 1 else 1 + 2 * NT, W)
+            cast_v(s - 2, cut_of(s - 2))
+            cast_s(s - 2, cut_of(s - 2))
+            store_bytes(s - 2)
+            if s == 3:
+                first_factor(1)
+                pick(0, 3, dot, 4, 1.0)
+                pick(1, 2, dot, 6, 1.0)
+                first_logit(2)
+                scale_of_pair(3)
+                first_logit(3)
+            if s == 5:
+                first_factor(2)
+                first_factor(3)
+            if 3 <= s <= nu:
+                factor(s - 1)

@@ -251,7 +251,7 @@ def tile_memorymoco_pa_kernel(tc, x0, x1, x2, x3, mem0, mem1, mem2, mem3, out_0,
 
         def column_zero(u):
             col = pair_col(u)
-            nc.gpsimd.tensor_copy(out=t_of[u][:, 0:1], in_=e0[:, col : col + 1])
+            nc.scalar.copy(out=t_of[u][:, 0:1], in_=e0[:, col : col + 1])
 
         def store(u, lo, hi):
             ci, m = units[u]
@@ -272,13 +272,16 @@ def tile_memorymoco_pa_kernel(tc, x0, x1, x2, x3, mem0, mem1, mem2, mem3, out_0,
             am_of[u] = small.tile([P, 1], F32, name="am")
             nc.vector.tensor_reduce(out=am_of[u][:], in_=t_of[u][:, 1:W], axis=AX.X, op=ALU.max)
 
-        def factor(u):
-            col = pair_col(u)
+        def invert(u):
             rc = small.tile([P, 1], F32, name="rc")
             nc.vector.reciprocal(out=rc[:], in_=am_of[u][:])
+            rc_of[u] = rc
+
+        def factor(u):
+            col = pair_col(u)
             r4 = small.tile([P, 1], F32, name="r4")
             r4_of[u] = r4
-            nc.gpsimd.tensor_scalar(out=r4[:], in0=rc[:], scalar1=448.0, scalar2=r0[:, col : col + 1], op0=ALU.mult, op1=ALU.min)
+            nc.vector.tensor_scalar(out=r4[:], in0=rc_of[u][:], scalar1=448.0, scalar2=r0[:, col : col + 1], op0=ALU.mult, op1=ALU.min)
 
         o8_of = {}
 
@@ -390,6 +393,8 @@ def tile_memorymoco_pa_kernel(tc, x0, x1, x2, x3, mem0, mem1, mem2, mem3, out_0,
         part_max(1, 3)
         fold_max(0)
         fold_max(1)
+        invert(0)
+        invert(1)
         factor(0)
         factor(1)
         gram(0, 2)
@@ -468,6 +473,8 @@ def tile_memorymoco_pa_kernel(tc, x0, x1, x2, x3, mem0, mem1, mem2, mem3, out_0,
                     first_exp(3)
                     column_zero(4)
                 store(s, 0 if s < nu - 1 else 1 + 2 * NT, W)
+            if 3 <= s <= nu:
+                invert(s - 1)
             cast_v(s - 2, cut_of(s - 2))
             cast_s(s - 2, cut_of(s - 2))
             store_bytes(s - 2)
@@ -478,7 +485,7 @@ def tile_memorymoco_pa_kernel(tc, x0, x1, x2, x3, mem0, mem1, mem2, mem3, out_0,
                 first_logit(2)
                 scale_of_pair(3)
                 first_logit(3)
-            if s == 5:
+            if s == 4:
                 first_factor(2)
                 first_factor(3)
             if 3 <= s <= nu:

@@ -429,7 +429,7 @@ def tile_memorymoco_pa_kernel(tc, x0, x1, x2, x3, mem0, mem1, mem2, mem3, out_0,
                 return 1344
             if u == nu - 2:
                 return 0
-            return 1600 if prep_of(u + 2) else 1280
+            return 1728 if prep_of(u + 2) else 1408
 
         def ahead(s, n):
             k = 4 * s + n + LEAD

@@ -59,6 +59,12 @@ def tile_memorymoco_pa_kernel(tc, x0, x1, x2, x3, mem0, mem1, mem2, mem3, out_0,
             xraw[v] = raw.tile([P, 2, D], BF16, name="xraw%d" % v)
             nc.sync.dma_start(out=xraw[v][:], in_=xs[v].rearrange("(m p) k -> p m k", p=P))
 
+        def load_chunk_halves(j, c):
+            mraw[(j, c)] = raw.tile([P, 4, D], BF16, name="mraw%d_%d" % (j, c))
+            rows = mems[j][NT * c : NT * (c + 1), :].rearrange("(p a) k -> p a k", p=P)
+            for h in range(2):
+                nc.sync.dma_start(out=mraw[(j, c)][:, 2 * h : 2 * h + 2, :], in_=rows[:, 2 * h : 2 * h + 2, :])
+
         def load_chunk(j, c):
             mraw[(j, c)] = raw.tile([P, 4, D], BF16, name="mraw%d_%d" % (j, c))
             nc.sync.dma_start(
@@ -66,9 +72,9 @@ def tile_memorymoco_pa_kernel(tc, x0, x1, x2, x3, mem0, mem1, mem2, mem3, out_0,
             )
 
         load_view(1)
-        load_chunk(0, 0)
+        load_chunk_halves(0, 0)
         load_view(0)
-        load_chunk(0, 1)
+        load_chunk_halves(0, 1)
         load_view(2)
         load_chunk(0, 2)
         load_chunk(0, 3)
@@ -92,10 +98,6 @@ def tile_memorymoco_pa_kernel(tc, x0, x1, x2, x3, mem0, mem1, mem2, mem3, out_0,
         rn = keep.tile([P, 8], F32, name="rn")
         dot = keep.tile([P, 8], F32, name="dot")
         sc = keep.tile([P, 8], F32, name="sc")
-        l0 = keep.tile([P, 8], F32, name="l0")
-        e0 = keep.tile([P, 8], F32, name="e0")
-        i0 = keep.tile([P, 8], F32, name="i0")
-        r0 = keep.tile([P, 8], F32, name="r0")
         junks = [keep.tile([P, D], F32, name="junk%d" % m) for m in range(2)]
 
 
@@ -177,28 +179,18 @@ def tile_memorymoco_pa_kernel(tc, x0, x1, x2, x3, mem0, mem1, mem2, mem3, out_0,
                     accum_out=dest[:, col + m : col + m + 1],
                 )
 
-        def inverse_lengths(v):
-            cols = slice(2 * v, 2 * v + 2)
-            nc.gpsimd.tensor_tensor(out=rn[:, cols], in0=ss[:, cols], in1=mhalf[:, 0:2], op=ALU.pow)
+        def inverse_lengths(v, lo=0, hi=2):
+            cols = slice(2 * v + lo, 2 * v + hi)
+            nc.gpsimd.tensor_tensor(out=rn[:, cols], in0=ss[:, cols], in1=mhalf[:, lo:hi], op=ALU.pow)
 
-        def scale_of_pair(pi):
+        def scale_of_pair(pi, lo=0, hi=2):
             i, j = PAIRS[pi]
             nc.gpsimd.tensor_tensor(
-                out=sc[:, 2 * pi : 2 * pi + 2], in0=rn[:, 2 * i : 2 * i + 2], in1=rn[:, 2 * j : 2 * j + 2], op=ALU.mult
+                out=sc[:, 2 * pi + lo : 2 * pi + hi],
+                in0=rn[:, 2 * i + lo : 2 * i + hi],
+                in1=rn[:, 2 * j + lo : 2 * j + hi],
+                op=ALU.mult,
             )
-
-        def first_logit(pi):
-            cols = slice(2 * pi, 2 * pi + 2)
-            nc.gpsimd.tensor_tensor(out=l0[:, cols], in0=dot[:, cols], in1=sc[:, cols], op=ALU.mult)
-
-        def first_exp(pi):
-            cols = slice(2 * pi, 2 * pi + 2)
-            nc.scalar.activation(out=e0[:, cols], in_=l0[:, cols], func=ACT.Exp)
-
-        def first_factor(pi):
-            cols = slice(2 * pi, 2 * pi + 2)
-            nc.vector.reciprocal(out=i0[:, cols], in_=e0[:, cols])
-            nc.gpsimd.tensor_scalar(out=r0[:, cols], in0=i0[:, cols], scalar1=448.0, scalar2=1.0, op0=ALU.mult, op1=ALU.mult)
 
         units = []
         for j in range(4):
@@ -251,7 +243,9 @@ def tile_memorymoco_pa_kernel(tc, x0, x1, x2, x3, mem0, mem1, mem2, mem3, out_0,
 
         def column_zero(u):
             col = pair_col(u)
-            nc.scalar.copy(out=t_of[u][:, 0:1], in_=e0[:, col : col + 1])
+            nc.scalar.activation(
+                out=t_of[u][:, 0:1], in_=dot[:, col : col + 1], func=ACT.Exp, scale=sc[:, col : col + 1]
+            )
 
         def store(u, lo, hi):
             ci, m = units[u]
@@ -272,16 +266,15 @@ def tile_memorymoco_pa_kernel(tc, x0, x1, x2, x3, mem0, mem1, mem2, mem3, out_0,
             am_of[u] = small.tile([P, 1], F32, name="am")
             nc.vector.tensor_reduce(out=am_of[u][:], in_=t_of[u][:, 1:W], axis=AX.X, op=ALU.max)
 
-        def invert(u):
-            rc = small.tile([P, 1], F32, name="rc")
-            nc.vector.reciprocal(out=rc[:], in_=am_of[u][:])
-            rc_of[u] = rc
+        def row_scale(u):
+            rc_of[u] = small.tile([P, 1], F32, name="rc")
+            nc.vector.tensor_scalar(
+                out=rc_of[u][:], in0=am_of[u][:], scalar1=t_of[u][:, 0:1], scalar2=1.0 / 448.0, op0=ALU.max, op1=ALU.mult
+            )
 
         def factor(u):
-            col = pair_col(u)
-            r4 = small.tile([P, 1], F32, name="r4")
-            r4_of[u] = r4
-            nc.vector.tensor_scalar(out=r4[:], in0=rc_of[u][:], scalar1=448.0, scalar2=r0[:, col : col + 1], op0=ALU.mult, op1=ALU.min)
+            r4_of[u] = small.tile([P, 1], F32, name="r4")
+            nc.vector.reciprocal(out=r4_of[u][:], in_=rc_of[u][:])
 
         o8_of = {}
 
@@ -314,23 +307,24 @@ def tile_memorymoco_pa_kernel(tc, x0, x1, x2, x3, mem0, mem1, mem2, mem3, out_0,
         inverse_lengths(1)
         move_view(1, sca)
         squares_from_rows(0, (0,))
+        inverse_lengths(0, 0, 1)
+        scale_of_pair(0, 0, 1)
         quantize_view(1)
         squares_from_rows(0, (1,))
-        inverse_lengths(0)
-        scale_of_pair(0)
+        inverse_lengths(0, 1, 2)
+        scale_of_pair(0, 1, 2)
         move_half(0, 0, 0, sca)
         move_half(0, 0, 1, sca)
         turn_half(0, 1, 0)
         turn_half(0, 1, 1)
-        dots_from_rows(0, 1, 0, (0,))
         quantize_chunk(0, 0)
+        dots_from_rows(0, 1, 0, (0,))
         dots_from_rows(0, 1, 0, (1,))
-        first_logit(0)
         move_half(0, 1, 0, sca)
         move_half(0, 1, 1, sca)
-        turn_view(2)
         product(0, 0)
         product(1, 0)
+        turn_view(2)
         squares_from_rows(2, (0,))
         quantize_chunk(0, 1)
         turn_half(0, 2, 0)
@@ -352,7 +346,6 @@ def tile_memorymoco_pa_kernel(tc, x0, x1, x2, x3, mem0, mem1, mem2, mem3, out_0,
         turn_view(3)
         exp_chunk(0, 1)
         exp_chunk(1, 1)
-        first_exp(0)
         column_zero(0)
         column_zero(1)
         product(0, 2)
@@ -381,7 +374,6 @@ def tile_memorymoco_pa_kernel(tc, x0, x1, x2, x3, mem0, mem1, mem2, mem3, out_0,
         product(2, 3)
         quantize_view(3)
         quantize_view(0)
-        first_factor(0)
         part_max(0, 2)
         part_max(1, 2)
         move_half(1, 0, 0, sca)
@@ -393,8 +385,8 @@ def tile_memorymoco_pa_kernel(tc, x0, x1, x2, x3, mem0, mem1, mem2, mem3, out_0,
         part_max(1, 3)
         fold_max(0)
         fold_max(1)
-        invert(0)
-        invert(1)
+        row_scale(0)
+        row_scale(1)
         factor(0)
         factor(1)
         gram(0, 2)
@@ -405,12 +397,11 @@ def tile_memorymoco_pa_kernel(tc, x0, x1, x2, x3, mem0, mem1, mem2, mem3, out_0,
         product(3, 0)
         turn_half(1, 1, 0)
         turn_half(1, 1, 1)
-        cast_v(0, 1600)
-        cast_s(0, 1600)
+        cast_v(0, 1728)
+        cast_s(0, 1728)
         store_bytes(0)
         pick(3, 3, ss, 6, TEMP)
         pick(0, 2, dot, 2, 1.0)
-        first_logit(1)
         inverse_lengths(3)
         scale_of_pair(2)
         quantize_chunk(1, 0)
@@ -429,7 +420,7 @@ def tile_memorymoco_pa_kernel(tc, x0, x1, x2, x3, mem0, mem1, mem2, mem3, out_0,
                 return 1344
             if u == nu - 2:
                 return 0
-            return 1728 if prep_of(u + 2) else 1408
+            return 1728 if prep_of(u + 2) else 896
 
         def ahead(s, n):
             k = 4 * s + n + LEAD
@@ -457,7 +448,6 @@ def tile_memorymoco_pa_kernel(tc, x0, x1, x2, x3, mem0, mem1, mem2, mem3, out_0,
                     exp_chunk(s, n)
                     ahead(s, n)
                     if n == 1 and s == 3:
-                        first_exp(1)
                         column_zero(2)
                         store(2, 0, W)
                         column_zero(3)
@@ -466,27 +456,17 @@ def tile_memorymoco_pa_kernel(tc, x0, x1, x2, x3, mem0, mem1, mem2, mem3, out_0,
                     if n == 1 and s == nu - 1:
                         column_zero(s)
                         store(s, 0, 1 + 2 * NT)
-                if 4 < s < nu - 1:
+                if 3 < s < nu - 1:
                     column_zero(s)
-                if s == 4:
-                    first_exp(2)
-                    first_exp(3)
-                    column_zero(4)
                 store(s, 0 if s < nu - 1 else 1 + 2 * NT, W)
             if 3 <= s <= nu:
-                invert(s - 1)
+                row_scale(s - 1)
             cast_v(s - 2, cut_of(s - 2))
             cast_s(s - 2, cut_of(s - 2))
             store_bytes(s - 2)
             if s == 3:
-                first_factor(1)
                 pick(0, 3, dot, 4, 1.0)
                 pick(1, 2, dot, 6, 1.0)
-                first_logit(2)
                 scale_of_pair(3)
-                first_logit(3)
-            if s == 4:
-                first_factor(2)
-                first_factor(3)
             if 3 <= s <= nu:
                 factor(s - 1)

@@ -1,3 +1,4 @@
+import math
 from contextlib import ExitStack
 
 import concourse.mybir as mybir
@@ -43,7 +44,7 @@ def tile_memorymoco_pa_kernel(tc, x0, x1, x2, x3, mem0, mem1, mem2, mem3, out_0,
 
         ident = const.tile([P, P], F32, name="ident")
         make_identity(nc, ident[:])
-        mhalf = const.tile([P, 4], F32, name="mhalf")
+        mhalf = const.tile([P, 2], F32, name="mhalf")
         nc.gpsimd.memset(mhalf[:], -0.5)
         zero = const.tile([P, 1], F32, name="zero")
         nc.vector.memset(zero[:], 0.0)
@@ -98,6 +99,7 @@ def tile_memorymoco_pa_kernel(tc, x0, x1, x2, x3, mem0, mem1, mem2, mem3, out_0,
         rn = keep.tile([P, 8], F32, name="rn")
         dot = keep.tile([P, 8], F32, name="dot")
         sc = keep.tile([P, 8], F32, name="sc")
+        junk_s = keep.tile([P, D], F32, name="junk_s")
         junks = [keep.tile([P, D], F32, name="junk%d" % m) for m in range(2)]
 
 
@@ -141,6 +143,12 @@ def tile_memorymoco_pa_kernel(tc, x0, x1, x2, x3, mem0, mem1, mem2, mem3, out_0,
             cols = slice(NT * c, NT * (c + 1))
             nc.vector.quantize_mx(out=mc[j][:, cols].bitcast(FP8X4), scales=msc[j][:, cols], in_=g_of[(j, c)][:])
 
+        def square_s(v, m):
+            nc.scalar.activation(
+                out=junk_s[:], in_=xraw[v][:, m, :], func=ACT.Square, scale=math.sqrt(TEMP),
+                accum_out=ss[:, 2 * v + m : 2 * v + m + 1],
+            )
+
         def squares_from_rows(v, halves=(0, 1)):
             for m in halves:
                 nc.vector.scalar_tensor_tensor(
@@ -179,17 +187,14 @@ def tile_memorymoco_pa_kernel(tc, x0, x1, x2, x3, mem0, mem1, mem2, mem3, out_0,
                     accum_out=dest[:, col + m : col + m + 1],
                 )
 
-        def inverse_lengths(v, lo=0, hi=2):
-            cols = slice(2 * v + lo, 2 * v + hi)
-            nc.gpsimd.tensor_tensor(out=rn[:, cols], in0=ss[:, cols], in1=mhalf[:, lo:hi], op=ALU.pow)
+        def inverse_lengths(v):
+            cols = slice(2 * v, 2 * v + 2)
+            nc.gpsimd.tensor_tensor(out=rn[:, cols], in0=ss[:, cols], in1=mhalf[:], op=ALU.pow)
 
-        def scale_of_pair(pi, lo=0, hi=2):
+        def scale_of_pair(pi):
             i, j = PAIRS[pi]
-            nc.gpsimd.tensor_tensor(
-                out=sc[:, 2 * pi + lo : 2 * pi + hi],
-                in0=rn[:, 2 * i + lo : 2 * i + hi],
-                in1=rn[:, 2 * j + lo : 2 * j + hi],
-                op=ALU.mult,
+            nc.vector.tensor_tensor(
+                out=sc[:, 2 * pi : 2 * pi + 2], in0=rn[:, 2 * i : 2 * i + 2], in1=rn[:, 2 * j : 2 * j + 2], op=ALU.mult
             )
 
         units = []
@@ -307,19 +312,17 @@ def tile_memorymoco_pa_kernel(tc, x0, x1, x2, x3, mem0, mem1, mem2, mem3, out_0,
         inverse_lengths(1)
         move_view(1, sca)
         squares_from_rows(0, (0,))
-        inverse_lengths(0, 0, 1)
-        scale_of_pair(0, 0, 1)
         quantize_view(1)
-        squares_from_rows(0, (1,))
-        inverse_lengths(0, 1, 2)
-        scale_of_pair(0, 1, 2)
         move_half(0, 0, 0, sca)
         move_half(0, 0, 1, sca)
+        square_s(0, 1)
+        inverse_lengths(0)
         turn_half(0, 1, 0)
         turn_half(0, 1, 1)
         quantize_chunk(0, 0)
         dots_from_rows(0, 1, 0, (0,))
         dots_from_rows(0, 1, 0, (1,))
+        scale_of_pair(0)
         move_half(0, 1, 0, sca)
         move_half(0, 1, 1, sca)
         product(0, 0)
@@ -336,7 +339,6 @@ def tile_memorymoco_pa_kernel(tc, x0, x1, x2, x3, mem0, mem1, mem2, mem3, out_0,
         move_view(2, vec)
         squares_from_rows(2, (1,))
         inverse_lengths(2)
-        scale_of_pair(1)
         quantize_view(2)
         move_half(0, 2, 0, sca)
         move_half(0, 2, 1, sca)
@@ -352,6 +354,7 @@ def tile_memorymoco_pa_kernel(tc, x0, x1, x2, x3, mem0, mem1, mem2, mem3, out_0,
         product(1, 2)
         product(2, 0)
         part_max(0, 0)
+        scale_of_pair(1)
         part_max(1, 0)
         move_half(0, 3, 0, sca)
         move_half(0, 3, 1, sca)
@@ -373,24 +376,28 @@ def tile_memorymoco_pa_kernel(tc, x0, x1, x2, x3, mem0, mem1, mem2, mem3, out_0,
         product(2, 2)
         product(2, 3)
         quantize_view(3)
+        squares_from_rows(3, (0,))
         quantize_view(0)
         part_max(0, 2)
         part_max(1, 2)
         move_half(1, 0, 0, sca)
+        square_s(3, 1)
         exp_chunk(0, 3)
         exp_chunk(1, 3)
+        inverse_lengths(3)
         store(0, 0, W)
         store(1, 0, W)
         part_max(0, 3)
         part_max(1, 3)
         fold_max(0)
         fold_max(1)
+        scale_of_pair(2)
+        scale_of_pair(3)
         row_scale(0)
         row_scale(1)
         factor(0)
         factor(1)
         gram(0, 2)
-        gram(3, 3)
         exp_chunk(2, 2)
         exp_chunk(2, 3)
         move_half(1, 0, 1, sca)
@@ -400,11 +407,9 @@ def tile_memorymoco_pa_kernel(tc, x0, x1, x2, x3, mem0, mem1, mem2, mem3, out_0,
         cast_v(0, 1728)
         cast_s(0, 1728)
         store_bytes(0)
-        pick(3, 3, ss, 6, TEMP)
         pick(0, 2, dot, 2, 1.0)
-        inverse_lengths(3)
-        scale_of_pair(2)
         quantize_chunk(1, 0)
+        row_max(2)
         product(3, 1)
         product(3, 2)
         product(3, 3)
@@ -435,7 +440,11 @@ def tile_memorymoco_pa_kernel(tc, x0, x1, x2, x3, mem0, mem1, mem2, mem3, out_0,
             if follow:
                 turn_half(follow[0], follow[1], 0)
                 turn_half(follow[0], follow[1], 1)
-            if s < nu:
+            if s == 5:
+                pick(0, 3, dot, 4, 1.0)
+            if s == 7:
+                pick(1, 2, dot, 6, 1.0)
+            if 3 < s < nu:
                 row_max(s - 1)
             elif s == nu:
                 for n in range(4):
@@ -451,22 +460,24 @@ def tile_memorymoco_pa_kernel(tc, x0, x1, x2, x3, mem0, mem1, mem2, mem3, out_0,
                         column_zero(2)
                         store(2, 0, W)
                         column_zero(3)
-                        gram(0, 3)
-                        gram(1, 2)
                     if n == 1 and s == nu - 1:
                         column_zero(s)
                         store(s, 0, 1 + 2 * NT)
-                if 3 < s < nu - 1:
+                if s == 5:
+                    column_zero(4)
+                    store(4, 0, W)
+                if 4 < s < nu - 1:
                     column_zero(s)
-                store(s, 0 if s < nu - 1 else 1 + 2 * NT, W)
+                if s != 4:
+                    store(s, 0 if s < nu - 1 else 1 + 2 * NT, W)
             if 3 <= s <= nu:
                 row_scale(s - 1)
             cast_v(s - 2, cut_of(s - 2))
             cast_s(s - 2, cut_of(s - 2))
             store_bytes(s - 2)
-            if s == 3:
-                pick(0, 3, dot, 4, 1.0)
-                pick(1, 2, dot, 6, 1.0)
-                scale_of_pair(3)
+            if s == 4:
+                gram(0, 3)
+            if s == 6:
+                gram(1, 2)
             if 3 <= s <= nu:
                 factor(s - 1)

@@ -156,13 +156,6 @@ def tile_memorymoco_pa_kernel(tc, x0, x1, x2, x3, mem0, mem1, mem2, mem3, out_0,
                     accum_out=ss[:, 2 * v + m : 2 * v + m + 1],
                 )
 
-        def dots_from_rows(i, j, pi, halves=(0, 1)):
-            for m in halves:
-                nc.vector.scalar_tensor_tensor(
-                    out=junks[m][:], in0=xraw[i][:, m, :], scalar=1.0, in1=xraw[j][:, m, :], op0=ALU.mult, op1=ALU.mult,
-                    accum_out=dot[:, 2 * pi + m : 2 * pi + m + 1],
-                )
-
         gb_of = {}
 
         def gram(i, j):
@@ -320,15 +313,13 @@ def tile_memorymoco_pa_kernel(tc, x0, x1, x2, x3, mem0, mem1, mem2, mem3, out_0,
         turn_half(0, 1, 0)
         turn_half(0, 1, 1)
         quantize_chunk(0, 0)
-        dots_from_rows(0, 1, 0, (0,))
-        dots_from_rows(0, 1, 0, (1,))
-        scale_of_pair(0)
         move_half(0, 1, 0, sca)
         move_half(0, 1, 1, sca)
         product(0, 0)
         product(1, 0)
         turn_view(2)
-        squares_from_rows(2, (0,))
+        squares_from_rows(2)
+        scale_of_pair(0)
         quantize_chunk(0, 1)
         turn_half(0, 2, 0)
         turn_half(0, 2, 1)
@@ -337,19 +328,16 @@ def tile_memorymoco_pa_kernel(tc, x0, x1, x2, x3, mem0, mem1, mem2, mem3, out_0,
         product(0, 1)
         product(1, 1)
         move_view(2, vec)
-        squares_from_rows(2, (1,))
         inverse_lengths(2)
         quantize_view(2)
         move_half(0, 2, 0, sca)
-        move_half(0, 2, 1, sca)
+        move_half(0, 2, 1, vec)
         quantize_chunk(0, 2)
         turn_half(0, 3, 0)
         turn_half(0, 3, 1)
         turn_view(3)
         exp_chunk(0, 1)
         exp_chunk(1, 1)
-        column_zero(0)
-        column_zero(1)
         product(0, 2)
         product(1, 2)
         product(2, 0)
@@ -385,31 +373,32 @@ def tile_memorymoco_pa_kernel(tc, x0, x1, x2, x3, mem0, mem1, mem2, mem3, out_0,
         exp_chunk(0, 3)
         exp_chunk(1, 3)
         inverse_lengths(3)
-        store(0, 0, W)
-        store(1, 0, W)
+        gram(0, 1)
         part_max(0, 3)
         part_max(1, 3)
+        pick(0, 1, dot, 0, 1.0)
         fold_max(0)
         fold_max(1)
         scale_of_pair(2)
         scale_of_pair(3)
-        row_scale(0)
-        row_scale(1)
-        factor(0)
-        factor(1)
-        gram(0, 2)
         exp_chunk(2, 2)
         exp_chunk(2, 3)
         move_half(1, 0, 1, sca)
+        column_zero(0)
+        column_zero(1)
+        store(0, 0, W)
+        store(1, 0, W)
         product(3, 0)
         turn_half(1, 1, 0)
         turn_half(1, 1, 1)
-        cast_v(0, 1728)
-        cast_s(0, 1728)
-        store_bytes(0)
-        pick(0, 2, dot, 2, 1.0)
+        gram(0, 2)
         quantize_chunk(1, 0)
+        row_scale(0)
+        row_scale(1)
         row_max(2)
+        factor(0)
+        factor(1)
+        pick(0, 2, dot, 2, 1.0)
         product(3, 1)
         product(3, 2)
         product(3, 3)
@@ -425,7 +414,7 @@ def tile_memorymoco_pa_kernel(tc, x0, x1, x2, x3, mem0, mem1, mem2, mem3, out_0,
                 return 1344
             if u == nu - 2:
                 return 0
-            return 1728 if prep_of(u + 2) else 896
+            return 1728 if prep_of(u + 3) else 1024
 
         def ahead(s, n):
             k = 4 * s + n + LEAD
@@ -456,7 +445,7 @@ def tile_memorymoco_pa_kernel(tc, x0, x1, x2, x3, mem0, mem1, mem2, mem3, out_0,
                 for n in range(4):
                     exp_chunk(s, n)
                     ahead(s, n)
-                    if n == 1 and s == 3:
+                    if n == 3 and s == 3:
                         column_zero(2)
                         store(2, 0, W)
                         column_zero(3)
@@ -472,9 +461,10 @@ def tile_memorymoco_pa_kernel(tc, x0, x1, x2, x3, mem0, mem1, mem2, mem3, out_0,
                     store(s, 0 if s < nu - 1 else 1 + 2 * NT, W)
             if 3 <= s <= nu:
                 row_scale(s - 1)
-            cast_v(s - 2, cut_of(s - 2))
-            cast_s(s - 2, cut_of(s - 2))
-            store_bytes(s - 2)
+            for u in (0, 1) if s == 3 else (s - 2,):
+                cast_v(u, cut_of(u))
+                cast_s(u, cut_of(u))
+                store_bytes(u)
             if s == 4:
                 gram(0, 3)
             if s == 6:

@@ -35,10 +35,10 @@ def tile_memorymoco_pa_kernel(tc, x0, x1, x2, x3, mem0, mem1, mem2, mem3, out_0,
         const = ctx.enter_context(tc.tile_pool(name="const", bufs=1))
         raw = ctx.enter_context(tc.tile_pool(name="raw", bufs=1))
         keep = ctx.enter_context(tc.tile_pool(name="keep", bufs=1))
-        grp = ctx.enter_context(tc.tile_pool(name="grp", bufs=3))
-        tpool = ctx.enter_context(tc.tile_pool(name="tpool", bufs=6))
-        opool = ctx.enter_context(tc.tile_pool(name="opool", bufs=4))
-        small = ctx.enter_context(tc.tile_pool(name="small", bufs=4))
+        grp = ctx.enter_context(tc.tile_pool(name="grp", bufs=4))
+        tpool = ctx.enter_context(tc.tile_pool(name="tpool", bufs=8))
+        opool = ctx.enter_context(tc.tile_pool(name="opool", bufs=6))
+        small = ctx.enter_context(tc.tile_pool(name="small", bufs=8))
         tps = ctx.enter_context(tc.psum_pool(name="tps", bufs=3))
         psum = ctx.enter_context(tc.psum_pool(name="psum", bufs=5))
 
@@ -284,6 +284,17 @@ def tile_memorymoco_pa_kernel(tc, x0, x1, x2, x3, mem0, mem1, mem2, mem3, out_0,
                     saturate=False,
                 )
 
+        def cast_v_last(u, cut):
+            ci, m = units[u]
+            o8_of[u] = opool.tile([P, W], FP8, name="o8")
+            for lo, hi in ((0, cut // 2), (cut // 2, cut)):
+                nc.vector.tensor_scalar(
+                    out=o8_of[u][:, lo:hi], in0=t_of[u][:, lo:hi], scalar1=r4_of[u][:, 0:1], scalar2=None, op0=ALU.mult,
+                    saturate=False,
+                )
+                if lo == 0:
+                    nc.sync.dma_start(out=out_1[ci, P * m : P * (m + 1), 0:hi], in_=o8_of[u][:, 0:hi].bitcast(U8))
+
         def cast_s(u, cut):
             if cut < W:
                 nc.scalar.activation(
@@ -291,9 +302,9 @@ def tile_memorymoco_pa_kernel(tc, x0, x1, x2, x3, mem0, mem1, mem2, mem3, out_0,
                     bias=zero[:, 0:1], saturate=False,
                 )
 
-        def store_bytes(u):
+        def store_bytes(u, lo=0):
             ci, m = units[u]
-            nc.sync.dma_start(out=out_1[ci, P * m : P * (m + 1), :], in_=o8_of[u][:].bitcast(U8))
+            nc.sync.dma_start(out=out_1[ci, P * m : P * (m + 1), lo:W], in_=o8_of[u][:, lo:W].bitcast(U8))
 
         sca = nc.scalar.copy
         vec = nc.vector.tensor_copy
@@ -411,10 +422,8 @@ def tile_memorymoco_pa_kernel(tc, x0, x1, x2, x3, mem0, mem1, mem2, mem3, out_0,
 
         def cut_of(u):
             if u == nu - 1:
-                return 1344
-            if u == nu - 2:
-                return 0
-            return 1728 if prep_of(u + 3) else 1024
+                return 1472
+            return 1728 if prep_of(u + 3) else 832
 
         def ahead(s, n):
             k = 4 * s + n + LEAD
@@ -461,6 +470,11 @@ def tile_memorymoco_pa_kernel(tc, x0, x1, x2, x3, mem0, mem1, mem2, mem3, out_0,
                     store(s, 0 if s < nu - 1 else 1 + 2 * NT, W)
             if 3 <= s <= nu:
                 row_scale(s - 1)
+            if s == nu + 1:
+                cast_v_last(nu - 1, cut_of(nu - 1))
+                cast_s(nu - 1, cut_of(nu - 1))
+                store_bytes(nu - 1, cut_of(nu - 1) // 2)
+                break
             for u in (0, 1) if s == 3 else (s - 2,):
                 cast_v(u, cut_of(u))
                 cast_s(u, cut_of(u))

import math
from contextlib import ExitStack

import concourse.mybir as mybir
from concourse.masks import make_identity

F32 = mybir.dt.float32
BF16 = mybir.dt.bfloat16
U32 = mybir.dt.uint32
U8 = mybir.dt.uint8
FP8X4 = mybir.dt.float8_e4m3fn_x4
FP8 = mybir.dt.float8_e4m3fn
ALU = mybir.AluOpType
ACT = mybir.ActivationFunctionType
AX = mybir.AxisListType

B, Q, D = 256, 2048, 512
COMBOS = ((0, 1), (0, 2), (0, 3), (1, 0), (1, 2), (2, 0), (2, 1), (3, 0))
TEMP = 0.07
FLOPS = 2 * len(COMBOS) * B * Q * D

P = 128
NT = 512
W = 1 + Q
PAIRS = ((0, 1), (0, 2), (0, 3), (1, 2))
BANK_ORDER = (0, 1, 2, 3)


def tile_memorymoco_pa_kernel(tc, x0, x1, x2, x3, mem0, mem1, mem2, mem3, out_0, out_1):
    nc = tc.nc
    xs = (x0, x1, x2, x3)
    mems = (mem0, mem1, mem2, mem3)

    with ExitStack() as ctx:
        const = ctx.enter_context(tc.tile_pool(name="const", bufs=1))
        raw = ctx.enter_context(tc.tile_pool(name="raw", bufs=1))
        keep = ctx.enter_context(tc.tile_pool(name="keep", bufs=1))
        grp = ctx.enter_context(tc.tile_pool(name="grp", bufs=4))
        tpool = ctx.enter_context(tc.tile_pool(name="tpool", bufs=8))
        opool = ctx.enter_context(tc.tile_pool(name="opool", bufs=6))
        small = ctx.enter_context(tc.tile_pool(name="small", bufs=8))
        tps = ctx.enter_context(tc.psum_pool(name="tps", bufs=3))
        psum = ctx.enter_context(tc.psum_pool(name="psum", bufs=5))

        ident = const.tile([P, P], F32, name="ident")
        make_identity(nc, ident[:])
        mhalf = const.tile([P, 2], F32, name="mhalf")
        nc.gpsimd.memset(mhalf[:], -0.5)
        zero = const.tile([P, 1], F32, name="zero")
        nc.vector.memset(zero[:], 0.0)
        warm = const.tile([P, 1], F32, name="warm")
        nc.scalar.activation(out=warm[:], in_=zero[:], func=ACT.Exp)

        ctx.enter_context(tc.manual_schedule())

        xraw = {}
        mraw = {}

        def load_view(v):
            xraw[v] = raw.tile([P, 2, D], BF16, name="xraw%d" % v)
            nc.sync.dma_start(out=xraw[v][:], in_=xs[v].rearrange("(m p) k -> p m k", p=P))

        def load_chunk_halves(j, c):
            mraw[(j, c)] = raw.tile([P, 4, D], BF16, name="mraw%d_%d" % (j, c))
            rows = mems[j][NT * c : NT * (c + 1), :].rearrange("(p a) k -> p a k", p=P)
            for h in range(2):
                nc.sync.dma_start(out=mraw[(j, c)][:, 2 * h : 2 * h + 2, :], in_=rows[:, 2 * h : 2 * h + 2, :])

        def load_chunk(j, c):
            mraw[(j, c)] = raw.tile([P, 4, D], BF16, name="mraw%d_%d" % (j, c))
            nc.sync.dma_start(
                out=mraw[(j, c)][:], in_=mems[j][NT * c : NT * (c + 1), :].rearrange("(p a) k -> p a k", p=P)
            )

        load_view(1)
        load_chunk_halves(0, 0)
        load_view(0)
        load_chunk_halves(0, 1)
        load_view(2)
        load_chunk(0, 2)
        load_chunk(0, 3)
        load_view(3)
        for j in BANK_ORDER[1:]:
            for c in range(4):
                load_chunk(j, c)

        gx = {}
        xc = {}
        xsc = {}
        mc = {}
        msc = {}
        for v in range(4):
            gx[v] = keep.tile([P, 4 * B], BF16, name="gx%d" % v, align_bytes=64)
            xc[v] = keep.tile([P, B], U32, name="xc%d" % v, align_bytes=64)
            xsc[v] = keep.tile([P, B], U8, name="xsc%d" % v, align_bytes=64)
            mc[v] = keep.tile([P, Q], U32, name="mc%d" % v, align_bytes=64)
            msc[v] = keep.tile([P, Q], U8, name="msc%d" % v, align_bytes=64)
        ss = keep.tile([P, 8], F32, name="ss")
        rn = keep.tile([P, 8], F32, name="rn")
        dot = keep.tile([P, 8], F32, name="dot")
        sc = keep.tile([P, 8], F32, name="sc")
        junk_s = keep.tile([P, D], F32, name="junk_s")
        junks = [keep.tile([P, D], F32, name="junk%d" % m) for m in range(2)]


        tp_of = {}

        def turn_view(v):
            tp = tps.tile([P, 2, 2, P], F32, name="tp")
            tp_of[("x", v)] = tp
            for m in range(2):
                words = xraw[v][:, m, :].bitcast(F32)
                for u in range(2):
                    nc.tensor.transpose(tp[:, m, u, :], words[:, u : D // 2 : 2], ident[:])

        def move_view(v, copy):
            copy(
                out=gx[v][:].bitcast(F32).rearrange("p (m r u) -> p m r u", m=2, u=2),
                in_=tp_of[("x", v)][:].rearrange("p m u r -> p m r u"),
            )

        def quantize_view(v):
            nc.vector.quantize_mx(out=xc[v][:].bitcast(FP8X4), scales=xsc[v][:], in_=gx[v][:])

        g_of = {}

        def turn_half(j, c, h):
            tp = tps.tile([P, 2, 2, P], F32, name="tp")
            tp_of[(j, c, h)] = tp
            for a in range(2):
                words = mraw[(j, c)][:, 2 * h + a, :].bitcast(F32)
                for u in range(2):
                    nc.tensor.transpose(tp[:, a, u, :], words[:, u : D // 2 : 2], ident[:])

        def move_half(j, c, h, copy):
            if h == 0:
                g_of[(j, c)] = grp.tile([P, 4 * NT], BF16, name="g", align_bytes=64)
            lo = 1024 * h
            dst = g_of[(j, c)][:, lo : lo + 1024].bitcast(F32).rearrange("p (a r u) -> p a r u", a=2, u=2)
            copy(out=dst, in_=tp_of[(j, c, h)][:].rearrange("p a u r -> p a r u"))

        def quantize_chunk(j, c):
            cols = slice(NT * c, NT * (c + 1))
            nc.vector.quantize_mx(out=mc[j][:, cols].bitcast(FP8X4), scales=msc[j][:, cols], in_=g_of[(j, c)][:])

        def square_s(v, m):
            nc.scalar.activation(
                out=junk_s[:], in_=xraw[v][:, m, :], func=ACT.Square, scale=math.sqrt(TEMP),
                accum_out=ss[:, 2 * v + m : 2 * v + m + 1],
            )

        def squares_from_rows(v, halves=(0, 1)):
            for m in halves:
                nc.vector.scalar_tensor_tensor(
                    out=junks[m][:], in0=xraw[v][:, m, :], scalar=TEMP, in1=xraw[v][:, m, :], op0=ALU.mult, op1=ALU.mult,
                    accum_out=ss[:, 2 * v + m : 2 * v + m + 1],
                )

        gb_of = {}

        def gram(i, j):
            gb = psum.tile([P, 2, P], F32, name="ps")
            gb_of[(i, j)] = gb
            gi = gx[i][:].rearrange("p (c t) -> p c t", t=4)
            gj = gx[j][:].rearrange("p (c t) -> p c t", t=4)
            for m in range(2):
                for t in range(4):
                    nc.tensor.matmul(
                        out=gb[:, m, :],
                        lhsT=gi[:, P * m : P * (m + 1), t],
                        rhs=gj[:, P * m : P * (m + 1), t],
                        start=(t == 0),
                        stop=(t == 3),
                    )

        def pick(i, j, dest, col, factor):
            for m in range(2):
                nc.vector.scalar_tensor_tensor(
                    out=junks[m][:, 0:P], in0=gb_of[(i, j)][:, m, :], scalar=factor, in1=ident[:], op0=ALU.mult, op1=ALU.mult,
                    accum_out=dest[:, col + m : col + m + 1],
                )

        def inverse_lengths(v):
            cols = slice(2 * v, 2 * v + 2)
            nc.gpsimd.tensor_tensor(out=rn[:, cols], in0=ss[:, cols], in1=mhalf[:], op=ALU.pow)

        def scale_of_pair(pi):
            i, j = PAIRS[pi]
            nc.vector.tensor_tensor(
                out=sc[:, 2 * pi : 2 * pi + 2], in0=rn[:, 2 * i : 2 * i + 2], in1=rn[:, 2 * j : 2 * j + 2], op=ALU.mult
            )

        units = []
        for j in range(4):
            for ci in range(len(COMBOS)):
                if COMBOS[ci][1] == j:
                    units.append((ci, 0))
                    units.append((ci, 1))
        nu = len(units)
        t_of = {}
        am_of = {}
        r4_of = {}
        rc_of = {}
        ps_of = {}
        parts_of = {}

        def pair_col(u):
            ci, m = units[u]
            i, j = COMBOS[ci]
            return 2 * PAIRS.index((min(i, j), max(i, j))) + m

        def product(u, n):
            if u >= nu:
                return
            ci, m = units[u]
            i, j = COMBOS[ci]
            rows = slice(P * m, P * (m + 1))
            cols = slice(NT * n, NT * (n + 1))
            ps = psum.tile([P, NT], F32, name="ps")
            ps_of[(u, n)] = ps
            nc.tensor.matmul_mx(
                out=ps[:],
                lhsT=xc[i][:, rows].bitcast(FP8X4),
                lhsT_scale=xsc[i][:, rows],
                rhs=mc[j][:, cols].bitcast(FP8X4),
                rhs_scale=msc[j][:, cols],
                start=True,
                stop=True,
            )

        def exp_chunk(u, n):
            if n == 0:
                t_of[u] = tpool.tile([P, W], F32, name="t")
            col = pair_col(u)
            nc.scalar.activation(
                out=t_of[u][:, 1 + NT * n : 1 + NT * (n + 1)].rearrange("p (r a) -> p r a", a=4),
                in_=ps_of[(u, n)][:].rearrange("p (a r) -> p r a", a=4),
                func=ACT.Exp,
                scale=sc[:, col : col + 1],
            )

        def column_zero(u):
            col = pair_col(u)
            nc.scalar.activation(
                out=t_of[u][:, 0:1], in_=dot[:, col : col + 1], func=ACT.Exp, scale=sc[:, col : col + 1]
            )

        def store(u, lo, hi):
            ci, m = units[u]
            nc.sync.dma_start(out=out_0[ci, P * m : P * (m + 1), lo:hi], in_=t_of[u][:, lo:hi])

        def part_max(u, n):
            if u not in parts_of:
                parts_of[u] = small.tile([P, 4], F32, name="parts")
            nc.vector.tensor_reduce(
                out=parts_of[u][:, n : n + 1], in_=t_of[u][:, 1 + NT * n : 1 + NT * (n + 1)], axis=AX.X, op=ALU.max
            )

        def fold_max(u):
            am_of[u] = small.tile([P, 1], F32, name="am")
            nc.vector.tensor_reduce(out=am_of[u][:], in_=parts_of[u][:], axis=AX.X, op=ALU.max)

        def row_max(u):
            am_of[u] = small.tile([P, 1], F32, name="am")
            nc.vector.tensor_reduce(out=am_of[u][:], in_=t_of[u][:, 1:W], axis=AX.X, op=ALU.max)

        def row_scale(u):
            rc_of[u] = small.tile([P, 1], F32, name="rc")
            nc.vector.tensor_scalar(
                out=rc_of[u][:], in0=am_of[u][:], scalar1=t_of[u][:, 0:1], scalar2=1.0 / 448.0, op0=ALU.max, op1=ALU.mult
            )

        def factor(u):
            r4_of[u] = small.tile([P, 1], F32, name="r4")
            nc.vector.reciprocal(out=r4_of[u][:], in_=rc_of[u][:])

        o8_of = {}

        def cast_v(u, cut):
            o8_of[u] = opool.tile([P, W], FP8, name="o8")
            if cut > 0:
                nc.vector.tensor_scalar(
                    out=o8_of[u][:, 0:cut], in0=t_of[u][:, 0:cut], scalar1=r4_of[u][:, 0:1], scalar2=None, op0=ALU.mult,
                    saturate=False,
                )

        def cast_v_last(u, cut):
            ci, m = units[u]
            o8_of[u] = opool.tile([P, W], FP8, name="o8")
            for lo, hi in ((0, cut // 2), (cut // 2, cut)):
                nc.vector.tensor_scalar(
                    out=o8_of[u][:, lo:hi], in0=t_of[u][:, lo:hi], scalar1=r4_of[u][:, 0:1], scalar2=None, op0=ALU.mult,
                    saturate=False,
                )
                if lo == 0:
                    nc.sync.dma_start(out=out_1[ci, P * m : P * (m + 1), 0:hi], in_=o8_of[u][:, 0:hi].bitcast(U8))

        def cast_s(u, cut):
            if cut < W:
                nc.scalar.activation(
                    out=o8_of[u][:, cut:W], in_=t_of[u][:, cut:W], func=ACT.Identity, scale=r4_of[u][:, 0:1],
                    bias=zero[:, 0:1], saturate=False,
                )

        def store_bytes(u, lo=0):
            ci, m = units[u]
            nc.sync.dma_start(out=out_1[ci, P * m : P * (m + 1), lo:W], in_=o8_of[u][:, lo:W].bitcast(U8))

        sca = nc.scalar.copy
        vec = nc.vector.tensor_copy

        turn_view(1)
        turn_half(0, 0, 0)
        turn_half(0, 0, 1)
        squares_from_rows(1)
        inverse_lengths(1)
        move_view(1, sca)
        squares_from_rows(0, (0,))
        quantize_view(1)
        move_half(0, 0, 0, sca)
        move_half(0, 0, 1, sca)
        square_s(0, 1)
        inverse_lengths(0)
        turn_half(0, 1, 0)
        turn_half(0, 1, 1)
        quantize_chunk(0, 0)
        move_half(0, 1, 0, sca)
        move_half(0, 1, 1, sca)
        product(0, 0)
        product(1, 0)
        turn_view(2)
        squares_from_rows(2)
        scale_of_pair(0)
        quantize_chunk(0, 1)
        turn_half(0, 2, 0)
        turn_half(0, 2, 1)
        exp_chunk(0, 0)
        exp_chunk(1, 0)
        product(0, 1)
        product(1, 1)
        move_view(2, vec)
        inverse_lengths(2)
        quantize_view(2)
        move_half(0, 2, 0, sca)
        move_half(0, 2, 1, vec)
        quantize_chunk(0, 2)
        turn_half(0, 3, 0)
        turn_half(0, 3, 1)
        turn_view(3)
        exp_chunk(0, 1)
        exp_chunk(1, 1)
        product(0, 2)
        product(1, 2)
        product(2, 0)
        part_max(0, 0)
        scale_of_pair(1)
        part_max(1, 0)
        move_half(0, 3, 0, sca)
        move_half(0, 3, 1, sca)
        turn_view(0)
        part_max(0, 1)
        part_max(1, 1)
        quantize_chunk(0, 3)
        exp_chunk(0, 2)
        exp_chunk(1, 2)
        product(2, 1)
        turn_half(1, 0, 0)
        product(0, 3)
        product(1, 3)
        exp_chunk(2, 0)
        exp_chunk(2, 1)
        move_view(3, vec)
        move_view(0, vec)
        turn_half(1, 0, 1)
        product(2, 2)
        product(2, 3)
        quantize_view(3)
        squares_from_rows(3, (0,))
        quantize_view(0)
        part_max(0, 2)
        part_max(1, 2)
        move_half(1, 0, 0, sca)
        square_s(3, 1)
        exp_chunk(0, 3)
        exp_chunk(1, 3)
        inverse_lengths(3)
        gram(0, 1)
        part_max(0, 3)
        part_max(1, 3)
        pick(0, 1, dot, 0, 1.0)
        fold_max(0)
        fold_max(1)
        scale_of_pair(2)
        scale_of_pair(3)
        exp_chunk(2, 2)
        exp_chunk(2, 3)
        move_half(1, 0, 1, sca)
        column_zero(0)
        column_zero(1)
        store(0, 0, W)
        store(1, 0, W)
        product(3, 0)
        turn_half(1, 1, 0)
        turn_half(1, 1, 1)
        gram(0, 2)
        quantize_chunk(1, 0)
        row_scale(0)
        row_scale(1)
        row_max(2)
        factor(0)
        factor(1)
        pick(0, 2, dot, 2, 1.0)
        product(3, 1)
        product(3, 2)
        product(3, 3)

        preps = [(j, c) for j in (1, 2, 3) for c in range(4)]
        LEAD = 4

        def prep_of(s):
            return preps[s - 2] if 2 <= s < 2 + len(preps) else None

        def cut_of(u):
            if u == nu - 1:
                return 1472
            return 1728 if prep_of(u + 3) else 832

        def ahead(s, n):
            k = 4 * s + n + LEAD
            product(k // 4, k % 4)

        for s in range(3, nu + 2):
            prep = prep_of(s)
            follow = prep_of(s + 1)
            if prep:
                move_half(prep[0], prep[1], 0, sca)
                move_half(prep[0], prep[1], 1, sca)
            if follow:
                turn_half(follow[0], follow[1], 0)
                turn_half(follow[0], follow[1], 1)
            if s == 5:
                pick(0, 3, dot, 4, 1.0)
            if s == 7:
                pick(1, 2, dot, 6, 1.0)
            if 3 < s < nu:
                row_max(s - 1)
            elif s == nu:
                for n in range(4):
                    part_max(s - 1, n)
                fold_max(s - 1)
            if prep:
                quantize_chunk(*prep)
            if s < nu:
                for n in range(4):
                    exp_chunk(s, n)
                    ahead(s, n)
                    if n == 3 and s == 3:
                        column_zero(2)
                        store(2, 0, W)
                        column_zero(3)
                    if n == 1 and s == nu - 1:
                        column_zero(s)
                        store(s, 0, 1 + 2 * NT)
                if s == 5:
                    column_zero(4)
                    store(4, 0, W)
                if 4 < s < nu - 1:
                    column_zero(s)
                if s != 4:
                    store(s, 0 if s < nu - 1 else 1 + 2 * NT, W)
            if 3 <= s <= nu:
                row_scale(s - 1)
            if s == nu + 1:
                cast_v_last(nu - 1, cut_of(nu - 1))
                cast_s(nu - 1, cut_of(nu - 1))
                store_bytes(nu - 1, cut_of(nu - 1) // 2)
                break
            for u in (0, 1) if s == 3 else (s - 2,):
                cast_v(u, cut_of(u))
                cast_s(u, cut_of(u))
                store_bytes(u)
            if s == 4:
                gram(0, 3)
            if s == 6:
                gram(1, 2)
            if 3 <= s <= nu:
                factor(s - 1)
